import numpy as np
import ml_dtypes


def mxq(x, axis, fmt="e4m3"):
    dtype, down = {"e4m3": (ml_dtypes.float8_e4m3fn, 7), "e5m2": (ml_dtypes.float8_e5m2, 14)}[fmt]
    v = np.moveaxis(np.asarray(x, np.float32).astype(ml_dtypes.bfloat16).astype(np.float64), axis, -1)
    blocks = v.reshape(v.shape[:-1] + (-1, 32))
    amax = np.abs(blocks).max(-1, keepdims=True)
    byte = np.maximum(np.where(amax > 0, np.frexp(amax)[1] - 1 + 127, 0) - down, 1)
    scale = np.exp2(byte - 127.0)
    codes = (blocks / scale).astype(np.float32).astype(dtype).astype(np.float64)
    return np.moveaxis((codes * scale).reshape(v.shape), -1, axis)


WIDE = False


def mx_kscale(k):
    if not WIDE:
        return np.ones(k)
    levels = np.array([10, -10, 5, -5, 0])
    a = np.random.permutation(np.resize(levels, k // 512 * 4)).reshape(k // 512, 4)
    idx = np.arange(k)
    return np.exp2(a[idx // 512, idx % 128 // 32])


BF16 = ml_dtypes.bfloat16


def bf(x):
    return np.asarray(x, np.float32).astype(BF16)


def f64(x):
    return np.asarray(x).astype(np.float64)


B, C, H, W, HID, VOCAB = 256, 3, 84, 84, 1024, 8192
EPS = 1e-8
BETA = 8


def setup_inputs():
    words = np.random.standard_normal((VOCAB, HID))
    gain = 0.5 + np.random.random((VOCAB, 1))
    near = np.random.randint(0, VOCAB, B)
    a = 0.6 + 0.35 * np.random.random((B, 1))
    q = 1.5 * (a * words[near] + np.sqrt(1.0 - a * a) * np.random.standard_normal((B, HID)))
    r = mx_kscale(HID)[np.arange(B) * HID // B][:, None]
    return {"q": bf(q * r), "word_embs": bf(words * gain), "beta": BETA}


def reference(q, word_embs, beta):
    q, e = f64(q), f64(word_embs)
    q_norm = np.sqrt((q * q).sum(-1, keepdims=True))
    e_norm = np.sqrt((e * e).sum(-1))[None, :]
    sims = (mxq(q, 1, "e4m3") @ mxq(e, 1, "e4m3").T) / (q_norm * e_norm + EPS)
    x = beta * sims
    p = np.exp(x - x.max(-1, keepdims=True))
    return (mxq(p, 1, "e4m3") @ mxq(e, 0, "e4m3")) / p.sum(-1, keepdims=True)

@@ -1,0 +1,326 @@
+import concourse.mybir as mybir
+from concourse.masks import make_identity
+
+FLOPS = 2 * 2 * 256 * 8192 * 1024
+
+F32 = mybir.dt.float32
+BF16 = mybir.dt.bfloat16
+U32 = mybir.dt.uint32
+U8 = mybir.dt.uint8
+FP8X4 = mybir.dt.float8_e4m3fn_x4
+ALU = mybir.AluOpType
+ACT = mybir.ActivationFunctionType
+AXIS = mybir.AxisListType
+
+P = 128
+PACK = 4
+K_PASS = P * PACK
+BANK = 512
+
+QUERIES = 256
+HID = 1024
+VOCAB = 8192
+Q_TILES = QUERIES // P
+H_PASSES = HID // K_PASS
+GROUPS = VOCAB // K_PASS
+H_HALVES = HID // BANK
+PAIR = 2
+EPS = 1e-8
+TINY = 1e-30
+
+
+def reciprocal_norm(nc, pool, sum_sq, width):
+    floored = pool.tile([P, width], F32)
+    nc.vector.tensor_scalar_max(out=floored[:], in0=sum_sq, scalar1=TINY)
+    guess = pool.tile([P, width], F32)
+    nc.scalar.activation(out=guess[:], in_=floored[:], func=ACT.Abs_reciprocal_sqrt)
+    return floored, guess
+
+
+def newton_step(nc, pool, floored, guess, width):
+    factor = pool.tile([P, width], F32)
+    nc.vector.tensor_mul(out=factor[:], in0=guess[:], in1=guess[:])
+    nc.vector.tensor_mul(out=factor[:], in0=factor[:], in1=floored[:])
+    nc.vector.tensor_scalar(out=factor[:], in0=factor[:], scalar1=-0.5, scalar2=1.5, op0=ALU.mult, op1=ALU.add)
+    recip = pool.tile([P, width], F32)
+    nc.vector.tensor_mul(out=recip[:], in0=guess[:], in1=factor[:])
+    return recip
+
+
+def tile_frozenhopfield_pa_kernel(tc, q, word_embs, beta, out):
+    nc = tc.nc
+    with tc.tile_pool(name="keep", bufs=1) as keep:
+        ident_f = keep.tile([P, P], F32)
+        make_identity(nc, ident_f[:])
+        ident_b = keep.tile([P, P], BF16)
+        make_identity(nc, ident_b[:])
+
+        x_sb = keep.tile([P, Q_TILES, VOCAB], F32)
+        e2_codes = keep.tile([P, GROUPS, HID], U32, align_bytes=64)
+        e2_scales = keep.tile([P, GROUPS, HID], U8, align_bytes=64)
+        q_codes = keep.tile([P, H_PASSES, QUERIES], U32, align_bytes=64)
+        q_scales = keep.tile([P, H_PASSES, QUERIES], U8, align_bytes=64)
+        neg_c_rows = keep.tile([P, QUERIES], F32)
+        x_scale = keep.tile([P, Q_TILES], F32)
+        neg_c = keep.tile([P, Q_TILES], F32)
+        part_max = keep.tile([P, Q_TILES, GROUPS], F32)
+        part_sum = keep.tile([P, Q_TILES, GROUPS // PAIR], F32)
+
+        with (
+            tc.tile_pool(name="stream", bufs=3) as stream,
+            tc.tile_pool(name="work", bufs=2) as work,
+            tc.tile_pool(name="stats", bufs=3) as stats,
+            tc.psum_pool(name="ps_xt", bufs=3) as ps_xt,
+            tc.psum_pool(name="ps_st", bufs=2) as ps_st,
+            tc.psum_pool(name="ps_yn", bufs=2) as ps_yn,
+        ):
+            q_raw = stream.tile([P, Q_TILES, HID], BF16, tag="e_raw")
+            nc.sync.dma_start(out=q_raw[:], in_=q.rearrange("(t p) h -> p t h", p=P))
+            q_words = q_raw[:].bitcast(F32)
+            q_sq = stats.tile([P, Q_TILES], F32)
+            for t in range(Q_TILES):
+                junk = work.tile([P, HID], BF16, tag="junk")
+                nc.scalar.activation(out=junk[:], in_=q_raw[:, t, :], func=ACT.Square, accum_out=q_sq[:, t : t + 1])
+            q_floored, q_guess = reciprocal_norm(nc, stats, q_sq[:], Q_TILES)
+            q_recip = newton_step(nc, stats, q_floored, q_guess, Q_TILES)
+            nc.vector.tensor_scalar_mul(out=x_scale[:], in0=q_recip[:], scalar1=float(beta))
+            nc.vector.tensor_scalar_mul(out=neg_c[:], in0=q_recip[:], scalar1=-EPS)
+            c_ps = ps_st.tile([P, QUERIES], F32, tag="st")
+            for t in range(Q_TILES):
+                nc.tensor.matmul(
+                    out=c_ps[:, t * P : (t + 1) * P],
+                    lhsT=neg_c[:, t : t + 1].to_broadcast([P, P]),
+                    rhs=ident_f[:],
+                    start=True,
+                    stop=True,
+                )
+            nc.vector.tensor_copy(out=neg_c_rows[:], in_=c_ps[:])
+
+            q_grouped = stream.tile([P, H_PASSES, QUERIES, PACK], BF16, tag="g1", align_bytes=64)
+            q_grouped_w = q_grouped[:].bitcast(F32)
+            for c in range(H_PASSES):
+                xt = ps_xt.tile([P, 2, QUERIES], F32, tag="xt")
+                for u in range(2):
+                    for t in range(Q_TILES):
+                        w0 = (2 * c + u) * P
+                        nc.tensor.transpose(xt[:, u, t * P : (t + 1) * P], q_words[:, t, w0 : w0 + P], ident_f[:])
+                nc.scalar.copy(out=q_grouped_w[:, c, :, :], in_=xt[:].rearrange("p u b -> p b u"))
+            nc.vector.quantize_mx(
+                out=q_codes[:].rearrange("p c b -> p (c b)").bitcast(FP8X4),
+                scales=q_scales[:].rearrange("p c b -> p (c b)"),
+                in_=q_grouped[:].rearrange("p c b t -> p (c b t)"),
+            )
+
+            e_raw = {}
+            e_norm = {}
+            g1 = {}
+            st = {}
+            g_t = {}
+            y_n = {}
+
+            def load(g):
+                e_raw[g] = stream.tile([P, PACK, HID], BF16, name="e_raw")
+                rows = word_embs[g * K_PASS : (g + 1) * K_PASS, :]
+                nc.sync.dma_start(out=e_raw[g][:], in_=rows.rearrange("(p j) h -> p j h", j=PACK))
+
+            def norms(g):
+                e_sq = stats.tile([P, PACK], F32)
+                for j in range(PACK):
+                    junk = work.tile([P, HID], BF16, tag="junk")
+                    nc.scalar.activation(out=junk[:], in_=e_raw[g][:, j, :], func=ACT.Square, accum_out=e_sq[:, j : j + 1])
+                e_norm[g] = reciprocal_norm(nc, stats, e_sq[:], PACK)
+
+            def transpose_words(g):
+                e_words = e_raw[g][:].bitcast(F32)
+                g1[g] = []
+                for c in range(H_PASSES):
+                    grouped = stream.tile([P, K_PASS, PACK], BF16, tag="g1", align_bytes=64)
+                    grouped_w = grouped[:].bitcast(F32)
+                    for jp in range(PACK // 2):
+                        xt = ps_xt.tile([P, 2, 2 * P], F32, tag="xt")
+                        for u in range(2):
+                            for jj in range(2):
+                                w0 = (2 * c + u) * P
+                                nc.tensor.transpose(
+                                    xt[:, u, jj * P : (jj + 1) * P], e_words[:, 2 * jp + jj, w0 : w0 + P], ident_f[:]
+                                )
+                        nc.scalar.copy(
+                            out=grouped_w[:, jp * 2 * P : (jp + 1) * 2 * P, :], in_=xt[:].rearrange("p u v -> p v u")
+                        )
+                    g1[g].append(grouped)
+
+            def regroup_for_second_matmul(g):
+                for hh in range(H_HALVES):
+                    cols = slice(hh * BANK, (hh + 1) * BANK)
+                    g2 = stream.tile([P, BANK, PACK], BF16, align_bytes=64)
+                    nc.vector.tensor_copy(
+                        out=g2[:].rearrange("p (c i) t -> p c t i", i=4),
+                        in_=e_raw[g][:, :, cols].rearrange("p t (c i) -> p c t i", i=4),
+                    )
+                    nc.vector.quantize_mx(
+                        out=e2_codes[:, g, cols].bitcast(FP8X4),
+                        scales=e2_scales[:, g, cols],
+                        in_=g2[:].rearrange("p h t -> p (h t)"),
+                    )
+
+            def first_matmul(g):
+                e1_codes = work.tile([P, H_PASSES, K_PASS], U32, align_bytes=64)
+                e1_scales = work.tile([P, H_PASSES, K_PASS], U8, align_bytes=64)
+                for c in range(H_PASSES):
+                    nc.vector.quantize_mx(
+                        out=e1_codes[:, c, :].bitcast(FP8X4),
+                        scales=e1_scales[:, c, :],
+                        in_=g1[g][c][:].rearrange("p v t -> p (v t)"),
+                    )
+                floored, guess = e_norm[g]
+                e_recip = newton_step(nc, stats, floored, guess, PACK)
+                e_recip_sq = stats.tile([P, PACK], F32)
+                nc.vector.tensor_mul(out=e_recip_sq[:], in0=e_recip[:], in1=e_recip[:])
+                g_t[g] = work.tile([P, PACK, QUERIES], F32, name="g_t")
+                for j in range(PACK):
+                    nc.vector.tensor_scalar(
+                        out=g_t[g][:, j, :],
+                        in0=neg_c_rows[:],
+                        scalar1=e_recip_sq[:, j : j + 1],
+                        scalar2=e_recip[:, j : j + 1],
+                        op0=ALU.mult,
+                        op1=ALU.add,
+                    )
+                st[g] = []
+                for jp in range(PACK // 2):
+                    s_t = ps_st.tile([P, 2, QUERIES], F32, tag="st")
+                    for jj in range(2):
+                        j = 2 * jp + jj
+                        for c in range(H_PASSES):
+                            nc.tensor.matmul_mx(
+                                out=s_t[:, jj, :],
+                                lhsT=e1_codes[:, c, j * P : (j + 1) * P].bitcast(FP8X4),
+                                lhsT_scale=e1_scales[:, c, j * P : (j + 1) * P],
+                                rhs=q_codes[:, c, :].bitcast(FP8X4),
+                                rhs_scale=q_scales[:, c, :],
+                                start=(c == 0),
+                                stop=(c == H_PASSES - 1),
+                            )
+                    st[g].append(s_t)
+
+            def normalise_and_turn(g):
+                y_t = work.tile([P, PACK, QUERIES], F32)
+                for jp in range(PACK // 2):
+                    nc.vector.tensor_tensor(
+                        out=y_t[:, 2 * jp : 2 * jp + 2, :], in0=st[g][jp][:], in1=g_t[g][:, 2 * jp : 2 * jp + 2, :], op=ALU.mult
+                    )
+                y_n[g] = []
+                for t in range(Q_TILES):
+                    turned = ps_yn.tile([P, BANK], F32, tag="yn")
+                    for j in range(PACK):
+                        nc.tensor.transpose(turned[:, j * P : (j + 1) * P], y_t[:, j, t * P : (t + 1) * P], ident_f[:])
+                    y_n[g].append(turned)
+
+            def keep_and_max(g):
+                for t in range(Q_TILES):
+                    nc.vector.tensor_scalar(
+                        out=x_sb[:, t, g * K_PASS : (g + 1) * K_PASS],
+                        in0=y_n[g][t][:],
+                        scalar1=x_scale[:, t : t + 1],
+                        scalar2=None,
+                        op0=ALU.mult,
+                        op1=ALU.max,
+                        accum_out=part_max[:, t, g : g + 1],
+                    )
+
+            load(0)
+            load(1)
+            for i in range(-2, GROUPS):
+                if i + 4 < GROUPS:
+                    load(i + 4)
+                if i >= 0:
+                    normalise_and_turn(i)
+                if 0 <= i + 1 < GROUPS:
+                    first_matmul(i + 1)
+                if i + 2 < GROUPS:
+                    norms(i + 2)
+                    transpose_words(i + 2)
+                    regroup_for_second_matmul(i + 2)
+                if i >= 0:
+                    keep_and_max(i)
+
+        with (
+            tc.tile_pool(name="late", bufs=1) as late,
+            tc.tile_pool(name="probs", bufs=4) as probs,
+            tc.tile_pool(name="turned", bufs=2) as turned_pool,
+            tc.psum_pool(name="ps_acc", bufs=1) as ps_acc,
+            tc.psum_pool(name="ps_pt", bufs=4) as ps_pt,
+        ):
+            p_codes = late.tile([P, GROUPS, QUERIES], U32, align_bytes=64)
+            p_scales = late.tile([P, GROUPS, QUERIES], U8, align_bytes=64)
+            neg_max = late.tile([P, Q_TILES], F32)
+            nc.vector.tensor_reduce(out=neg_max[:], in_=part_max[:], axis=AXIS.X, op=ALU.max)
+            nc.vector.tensor_scalar_mul(out=neg_max[:], in0=neg_max[:], scalar1=-1.0)
+            acc = {}
+            for t in range(Q_TILES):
+                for hh in range(H_HALVES):
+                    acc[(t, hh)] = ps_acc.tile([P, BANK], F32, name="acc%d%d" % (t, hh))
+
+            p_bf = {}
+
+            def exponentials(u):
+                cols = slice(u * PAIR * K_PASS, (u + 1) * PAIR * K_PASS)
+                for t in range(Q_TILES):
+                    p_bf[(u, t)] = probs.tile([P, PAIR * K_PASS], BF16, name="p_bf")
+                    nc.scalar.activation(
+                        out=p_bf[(u, t)][:],
+                        in_=x_sb[:, t, cols],
+                        func=ACT.Exp,
+                        bias=neg_max[:, t : t + 1],
+                        scale=1.0,
+                        accum_out=part_sum[:, t, u : u + 1],
+                    )
+
+            def turn_and_quantise(u):
+                p_grouped = turned_pool.tile([P, PAIR, QUERIES, PACK], BF16, align_bytes=64)
+                for gl in range(PAIR):
+                    p_t = ps_pt.tile([P, PACK, QUERIES], BF16, tag="pt")
+                    for j in range(PACK):
+                        for t in range(Q_TILES):
+                            v0 = (gl * PACK + j) * P
+                            nc.tensor.transpose(p_t[:, j, t * P : (t + 1) * P], p_bf[(u, t)][:, v0 : v0 + P], ident_b[:])
+                    nc.vector.tensor_copy(out=p_grouped[:, gl, :, :], in_=p_t[:].rearrange("p j b -> p b j"))
+                nc.vector.quantize_mx(
+                    out=p_codes[:, u * PAIR : (u + 1) * PAIR, :].rearrange("p g b -> p (g b)").bitcast(FP8X4),
+                    scales=p_scales[:, u * PAIR : (u + 1) * PAIR, :].rearrange("p g b -> p (g b)"),
+                    in_=p_grouped[:].rearrange("p g b t -> p (g b t)"),
+                )
+
+            def second_matmul(u):
+                for g in range(u * PAIR, (u + 1) * PAIR):
+                    for t in range(Q_TILES):
+                        for hh in range(H_HALVES):
+                            nc.tensor.matmul_mx(
+                                out=acc[(t, hh)][:],
+                                lhsT=p_codes[:, g, t * P : (t + 1) * P].bitcast(FP8X4),
+                                lhsT_scale=p_scales[:, g, t * P : (t + 1) * P],
+                                rhs=e2_codes[:, g, hh * BANK : (hh + 1) * BANK].bitcast(FP8X4),
+                                rhs_scale=e2_scales[:, g, hh * BANK : (hh + 1) * BANK],
+                                start=(g == 0),
+                                stop=(g == GROUPS - 1),
+                            )
+
+            units = GROUPS // PAIR
+            exponentials(0)
+            for u in range(units + 1):
+                if u + 1 < units:
+                    exponentials(u + 1)
+                if u < units:
+                    turn_and_quantise(u)
+                if u >= 1:
+                    second_matmul(u - 1)
+
+            row_sum = late.tile([P, Q_TILES], F32)
+            nc.vector.tensor_reduce(out=row_sum[:], in_=part_sum[:], axis=AXIS.X, op=ALU.add)
+            inv_sum = late.tile([P, Q_TILES], F32)
+            nc.vector.reciprocal(out=inv_sum[:], in_=row_sum[:])
+            for t in range(Q_TILES):
+                result = probs.tile([P, HID], F32)
+                nc.vector.tensor_scalar_mul(out=result[:, 0:BANK], in0=acc[(t, 0)][:], scalar1=inv_sum[:, t : t + 1])
+                nc.scalar.activation(out=result[:, BANK:HID], in_=acc[(t, 1)][:], func=ACT.Copy, scale=inv_sum[:, t : t + 1])
+                nc.sync.dma_start(out=out[t * P : (t + 1) * P, :], in_=result[:])

@@ -27,29 +27,27 @@ H_HALVES = HID // BANK
 PAIR = 2
 EPS = 1e-8
 TINY = 1e-30
+LATE = 6
 
 
-def reciprocal_norm(nc, pool, sum_sq, width):
-    floored = pool.tile([P, width], F32)
-    nc.vector.tensor_scalar_max(out=floored[:], in0=sum_sq, scalar1=TINY)
+def rough_reciprocal_norm(nc, pool, sum_sq, width):
     guess = pool.tile([P, width], F32)
-    nc.scalar.activation(out=guess[:], in_=floored[:], func=ACT.Abs_reciprocal_sqrt)
-    return floored, guess
+    nc.scalar.activation(out=guess[:], in_=sum_sq, func=ACT.Abs_reciprocal_sqrt, bias=TINY)
+    return guess
 
 
-def newton_step(nc, pool, floored, guess, width):
+def newton_step(nc, pool, sum_sq, guess, width):
     factor = pool.tile([P, width], F32)
-    nc.vector.tensor_mul(out=factor[:], in0=guess[:], in1=guess[:])
-    nc.vector.tensor_mul(out=factor[:], in0=factor[:], in1=floored[:])
-    nc.vector.tensor_scalar(out=factor[:], in0=factor[:], scalar1=-0.5, scalar2=1.5, op0=ALU.mult, op1=ALU.add)
+    nc.vector.scalar_tensor_tensor(out=factor[:], in0=guess[:], scalar=-0.5, in1=guess[:], op0=ALU.mult, op1=ALU.mult)
+    nc.vector.tensor_mul(out=factor[:], in0=factor[:], in1=sum_sq)
     recip = pool.tile([P, width], F32)
-    nc.vector.tensor_mul(out=recip[:], in0=guess[:], in1=factor[:])
+    nc.vector.scalar_tensor_tensor(out=recip[:], in0=factor[:], scalar=1.5, in1=guess[:], op0=ALU.add, op1=ALU.mult)
     return recip
 
 
 def tile_frozenhopfield_pa_kernel(tc, q, word_embs, beta, out):
     nc = tc.nc
-    with tc.tile_pool(name="keep", bufs=1) as keep:
+    with tc.tile_pool(name="keep", bufs=1) as keep, tc.tile_pool(name="stream", bufs=3) as stream:
         ident_f = keep.tile([P, P], F32)
         make_identity(nc, ident_f[:])
         ident_b = keep.tile([P, P], BF16)
@@ -66,8 +64,29 @@ def tile_frozenhopfield_pa_kernel(tc, q, word_embs, beta, out):
         part_max = keep.tile([P, Q_TILES, GROUPS], F32)
         part_sum = keep.tile([P, Q_TILES, GROUPS // PAIR], F32)
 
+        e_raw = {}
+
+        def load(g):
+            e_raw[g] = stream.tile([P, PACK, HID], BF16, name="e_raw")
+            rows = word_embs[g * K_PASS : (g + 1) * K_PASS, :]
+            nc.sync.dma_start(out=e_raw[g][:], in_=rows.rearrange("(p j) h -> p j h", j=PACK))
+
+        def regroup_for_second_matmul(g):
+            for hh in range(H_HALVES):
+                cols = slice(hh * BANK, (hh + 1) * BANK)
+                g2 = stream.tile([P, BANK, PACK], BF16, align_bytes=64)
+                nc.vector.tensor_copy(
+                    out=g2[:].rearrange("p (c i) t -> p c t i", i=4),
+                    in_=e_raw[g][:, :, cols].rearrange("p t (c i) -> p c t i", i=4),
+                )
+                nc.vector.quantize_mx(
+                    out=e2_codes[:, g, cols].bitcast(FP8X4),
+                    scales=e2_scales[:, g, cols],
+                    in_=g2[:].rearrange("p h t -> p (h t)"),
+                )
+
         with (
-            tc.tile_pool(name="stream", bufs=3) as stream,
+            tc.tile_pool(name="grouped", bufs=3) as grouped_pool,
             tc.tile_pool(name="work", bufs=2) as work,
             tc.tile_pool(name="stats", bufs=3) as stats,
             tc.psum_pool(name="ps_xt", bufs=3) as ps_xt,
@@ -81,8 +100,8 @@ def tile_frozenhopfield_pa_kernel(tc, q, word_embs, beta, out):
             for t in range(Q_TILES):
                 junk = work.tile([P, HID], BF16, tag="junk")
                 nc.scalar.activation(out=junk[:], in_=q_raw[:, t, :], func=ACT.Square, accum_out=q_sq[:, t : t + 1])
-            q_floored, q_guess = reciprocal_norm(nc, stats, q_sq[:], Q_TILES)
-            q_recip = newton_step(nc, stats, q_floored, q_guess, Q_TILES)
+            q_guess = rough_reciprocal_norm(nc, stats, q_sq[:], Q_TILES)
+            q_recip = newton_step(nc, stats, q_sq[:], q_guess, Q_TILES)
             nc.vector.tensor_scalar_mul(out=x_scale[:], in0=q_recip[:], scalar1=float(beta))
             nc.vector.tensor_scalar_mul(out=neg_c[:], in0=q_recip[:], scalar1=-EPS)
             c_ps = ps_st.tile([P, QUERIES], F32, tag="st")
@@ -96,7 +115,7 @@ def tile_frozenhopfield_pa_kernel(tc, q, word_embs, beta, out):
                 )
             nc.vector.tensor_copy(out=neg_c_rows[:], in_=c_ps[:])
 
-            q_grouped = stream.tile([P, H_PASSES, QUERIES, PACK], BF16, tag="g1", align_bytes=64)
+            q_grouped = grouped_pool.tile([P, H_PASSES, QUERIES, PACK], BF16, tag="g1", align_bytes=64)
             q_grouped_w = q_grouped[:].bitcast(F32)
             for c in range(H_PASSES):
                 xt = ps_xt.tile([P, 2, QUERIES], F32, tag="xt")
@@ -111,30 +130,24 @@ def tile_frozenhopfield_pa_kernel(tc, q, word_embs, beta, out):
                 in_=q_grouped[:].rearrange("p c b t -> p (c b t)"),
             )
 
-            e_raw = {}
             e_norm = {}
             g1 = {}
             st = {}
             g_t = {}
             y_n = {}
 
-            def load(g):
-                e_raw[g] = stream.tile([P, PACK, HID], BF16, name="e_raw")
-                rows = word_embs[g * K_PASS : (g + 1) * K_PASS, :]
-                nc.sync.dma_start(out=e_raw[g][:], in_=rows.rearrange("(p j) h -> p j h", j=PACK))
-
             def norms(g):
                 e_sq = stats.tile([P, PACK], F32)
                 for j in range(PACK):
                     junk = work.tile([P, HID], BF16, tag="junk")
                     nc.scalar.activation(out=junk[:], in_=e_raw[g][:, j, :], func=ACT.Square, accum_out=e_sq[:, j : j + 1])
-                e_norm[g] = reciprocal_norm(nc, stats, e_sq[:], PACK)
+                e_norm[g] = (e_sq, rough_reciprocal_norm(nc, stats, e_sq[:], PACK))
 
             def transpose_words(g):
                 e_words = e_raw[g][:].bitcast(F32)
                 g1[g] = []
                 for c in range(H_PASSES):
-                    grouped = stream.tile([P, K_PASS, PACK], BF16, tag="g1", align_bytes=64)
+                    grouped = grouped_pool.tile([P, K_PASS, PACK], BF16, tag="g1", align_bytes=64)
                     grouped_w = grouped[:].bitcast(F32)
                     for jp in range(PACK // 2):
                         xt = ps_xt.tile([P, 2, 2 * P], F32, tag="xt")
@@ -144,24 +157,9 @@ def tile_frozenhopfield_pa_kernel(tc, q, word_embs, beta, out):
                                 nc.tensor.transpose(
                                     xt[:, u, jj * P : (jj + 1) * P], e_words[:, 2 * jp + jj, w0 : w0 + P], ident_f[:]
                                 )
-                        nc.scalar.copy(
-                            out=grouped_w[:, jp * 2 * P : (jp + 1) * 2 * P, :], in_=xt[:].rearrange("p u v -> p v u")
-                        )
+                        copy_out = nc.vector.tensor_copy if (c, jp) == (H_PASSES - 1, 1) else nc.scalar.copy
+                        copy_out(out=grouped_w[:, jp * 2 * P : (jp + 1) * 2 * P, :], in_=xt[:].rearrange("p u v -> p v u"))
                     g1[g].append(grouped)
-
-            def regroup_for_second_matmul(g):
-                for hh in range(H_HALVES):
-                    cols = slice(hh * BANK, (hh + 1) * BANK)
-                    g2 = stream.tile([P, BANK, PACK], BF16, align_bytes=64)
-                    nc.vector.tensor_copy(
-                        out=g2[:].rearrange("p (c i) t -> p c t i", i=4),
-                        in_=e_raw[g][:, :, cols].rearrange("p t (c i) -> p c t i", i=4),
-                    )
-                    nc.vector.quantize_mx(
-                        out=e2_codes[:, g, cols].bitcast(FP8X4),
-                        scales=e2_scales[:, g, cols],
-                        in_=g2[:].rearrange("p h t -> p (h t)"),
-                    )
 
             def first_matmul(g):
                 e1_codes = work.tile([P, H_PASSES, K_PASS], U32, align_bytes=64)
@@ -172,8 +170,8 @@ def tile_frozenhopfield_pa_kernel(tc, q, word_embs, beta, out):
                         scales=e1_scales[:, c, :],
                         in_=g1[g][c][:].rearrange("p v t -> p (v t)"),
                     )
-                floored, guess = e_norm[g]
-                e_recip = newton_step(nc, stats, floored, guess, PACK)
+                e_sq, guess = e_norm[g]
+                e_recip = newton_step(nc, stats, e_sq[:], guess, PACK)
                 e_recip_sq = stats.tile([P, PACK], F32)
                 nc.vector.tensor_mul(out=e_recip_sq[:], in0=e_recip[:], in1=e_recip[:])
                 g_t[g] = work.tile([P, PACK, QUERIES], F32, name="g_t")
@@ -240,7 +238,8 @@ def tile_frozenhopfield_pa_kernel(tc, q, word_embs, beta, out):
                 if i + 2 < GROUPS:
                     norms(i + 2)
                     transpose_words(i + 2)
-                    regroup_for_second_matmul(i + 2)
+                    if i + 2 < GROUPS - LATE:
+                        regroup_for_second_matmul(i + 2)
                 if i >= 0:
                     keep_and_max(i)
 
@@ -284,7 +283,8 @@ def tile_frozenhopfield_pa_kernel(tc, q, word_embs, beta, out):
                         for t in range(Q_TILES):
                             v0 = (gl * PACK + j) * P
                             nc.tensor.transpose(p_t[:, j, t * P : (t + 1) * P], p_bf[(u, t)][:, v0 : v0 + P], ident_b[:])
-                    nc.vector.tensor_copy(out=p_grouped[:, gl, :, :], in_=p_t[:].rearrange("p j b -> p b j"))
+                    copy_out = nc.vector.tensor_copy if gl == 0 else nc.scalar.copy
+                    copy_out(out=p_grouped[:, gl, :, :], in_=p_t[:].rearrange("p j b -> p b j"))
                 nc.vector.quantize_mx(
                     out=p_codes[:, u * PAIR : (u + 1) * PAIR, :].rearrange("p g b -> p (g b)").bitcast(FP8X4),
                     scales=p_scales[:, u * PAIR : (u + 1) * PAIR, :].rearrange("p g b -> p (g b)"),
@@ -306,12 +306,18 @@ def tile_frozenhopfield_pa_kernel(tc, q, word_embs, beta, out):
                             )
 
             units = GROUPS // PAIR
+            for g in range(GROUPS - LATE, GROUPS - LATE + 3):
+                load(g)
             exponentials(0)
             for u in range(units + 1):
                 if u + 1 < units:
                     exponentials(u + 1)
                 if u < units:
                     turn_and_quantise(u)
+                if u < LATE:
+                    regroup_for_second_matmul(GROUPS - LATE + u)
+                    if u + 3 < LATE:
+                        load(GROUPS - LATE + u + 3)
                 if u >= 1:
                     second_matmul(u - 1)
 

@@ -30,18 +30,11 @@ TINY = 1e-30
 LATE = 6
 
 
-def rough_reciprocal_norm(nc, pool, sum_sq, width):
-    guess = pool.tile([P, width], F32)
-    nc.scalar.activation(out=guess[:], in_=sum_sq, func=ACT.Abs_reciprocal_sqrt, bias=TINY)
-    return guess
-
-
-def newton_step(nc, pool, sum_sq, guess, width):
-    factor = pool.tile([P, width], F32)
-    nc.vector.scalar_tensor_tensor(out=factor[:], in0=guess[:], scalar=-0.5, in1=guess[:], op0=ALU.mult, op1=ALU.mult)
-    nc.vector.tensor_mul(out=factor[:], in0=factor[:], in1=sum_sq)
+def reciprocal_norm(nc, pool, sum_sq, minus_half, width):
+    shifted = pool.tile([P, width], F32)
+    nc.gpsimd.tensor_scalar(out=shifted[:], in0=sum_sq, scalar1=1.0, scalar2=TINY, op0=ALU.mult, op1=ALU.add)
     recip = pool.tile([P, width], F32)
-    nc.vector.scalar_tensor_tensor(out=recip[:], in0=factor[:], scalar=1.5, in1=guess[:], op0=ALU.add, op1=ALU.mult)
+    nc.gpsimd.tensor_tensor(out=recip[:], in0=shifted[:], in1=minus_half, op=ALU.pow)
     return recip
 
 
@@ -50,8 +43,9 @@ def tile_frozenhopfield_pa_kernel(tc, q, word_embs, beta, out):
     with tc.tile_pool(name="keep", bufs=1) as keep, tc.tile_pool(name="stream", bufs=3) as stream:
         ident_f = keep.tile([P, P], F32)
         make_identity(nc, ident_f[:])
-        ident_b = keep.tile([P, P], BF16)
-        make_identity(nc, ident_b[:])
+
+        minus_half = keep.tile([P, PACK], F32)
+        nc.gpsimd.memset(minus_half[:], -0.5)
 
         x_sb = keep.tile([P, Q_TILES, VOCAB], F32)
         e2_codes = keep.tile([P, GROUPS, HID], U32, align_bytes=64)
@@ -65,6 +59,7 @@ def tile_frozenhopfield_pa_kernel(tc, q, word_embs, beta, out):
         part_sum = keep.tile([P, Q_TILES, GROUPS // PAIR], F32)
 
         e_raw = {}
+        regrouped = {}
 
         def load(g):
             e_raw[g] = stream.tile([P, PACK, HID], BF16, name="e_raw")
@@ -72,6 +67,7 @@ def tile_frozenhopfield_pa_kernel(tc, q, word_embs, beta, out):
             nc.sync.dma_start(out=e_raw[g][:], in_=rows.rearrange("(p j) h -> p j h", j=PACK))
 
         def regroup_for_second_matmul(g):
+            regrouped[g] = []
             for hh in range(H_HALVES):
                 cols = slice(hh * BANK, (hh + 1) * BANK)
                 g2 = stream.tile([P, BANK, PACK], BF16, align_bytes=64)
@@ -79,69 +75,113 @@ def tile_frozenhopfield_pa_kernel(tc, q, word_embs, beta, out):
                     out=g2[:].rearrange("p (c i) t -> p c t i", i=4),
                     in_=e_raw[g][:, :, cols].rearrange("p t (c i) -> p c t i", i=4),
                 )
+                regrouped[g].append(g2)
+
+        def quantise_for_second_matmul(g):
+            for hh in range(H_HALVES):
+                cols = slice(hh * BANK, (hh + 1) * BANK)
                 nc.vector.quantize_mx(
                     out=e2_codes[:, g, cols].bitcast(FP8X4),
                     scales=e2_scales[:, g, cols],
-                    in_=g2[:].rearrange("p h t -> p (h t)"),
+                    in_=regrouped[g][hh][:].rearrange("p h t -> p (h t)"),
                 )
 
         with (
-            tc.tile_pool(name="grouped", bufs=3) as grouped_pool,
+            tc.tile_pool(name="grouped", bufs=4) as grouped_pool,
             tc.tile_pool(name="work", bufs=2) as work,
             tc.tile_pool(name="stats", bufs=3) as stats,
             tc.psum_pool(name="ps_xt", bufs=3) as ps_xt,
             tc.psum_pool(name="ps_st", bufs=2) as ps_st,
             tc.psum_pool(name="ps_yn", bufs=2) as ps_yn,
+            tc.psum_pool(name="ps_gram", bufs=1) as ps_gram,
         ):
-            q_raw = stream.tile([P, Q_TILES, HID], BF16, tag="e_raw")
-            nc.sync.dma_start(out=q_raw[:], in_=q.rearrange("(t p) h -> p t h", p=P))
-            q_words = q_raw[:].bitcast(F32)
-            q_sq = stats.tile([P, Q_TILES], F32)
-            for t in range(Q_TILES):
-                junk = work.tile([P, HID], BF16, tag="junk")
-                nc.scalar.activation(out=junk[:], in_=q_raw[:, t, :], func=ACT.Square, accum_out=q_sq[:, t : t + 1])
-            q_guess = rough_reciprocal_norm(nc, stats, q_sq[:], Q_TILES)
-            q_recip = newton_step(nc, stats, q_sq[:], q_guess, Q_TILES)
-            nc.vector.tensor_scalar_mul(out=x_scale[:], in0=q_recip[:], scalar1=float(beta))
-            nc.vector.tensor_scalar_mul(out=neg_c[:], in0=q_recip[:], scalar1=-EPS)
-            c_ps = ps_st.tile([P, QUERIES], F32, tag="st")
-            for t in range(Q_TILES):
-                nc.tensor.matmul(
-                    out=c_ps[:, t * P : (t + 1) * P],
-                    lhsT=neg_c[:, t : t + 1].to_broadcast([P, P]),
-                    rhs=ident_f[:],
-                    start=True,
-                    stop=True,
+            q_raw = work.tile([P, Q_TILES, HID], BF16, tag="y_t")
+
+            def quantise_queries():
+                q_words = q_raw[:].bitcast(F32)
+                q_grouped = grouped_pool.tile([P, H_PASSES, QUERIES, PACK], BF16, tag="g1", align_bytes=64)
+                q_grouped_w = q_grouped[:].bitcast(F32)
+                for c in range(H_PASSES):
+                    xt = ps_xt.tile([P, 2, QUERIES], F32, tag="xt")
+                    for u in range(2):
+                        for t in range(Q_TILES):
+                            w0 = (2 * c + u) * P
+                            nc.tensor.transpose(xt[:, u, t * P : (t + 1) * P], q_words[:, t, w0 : w0 + P], ident_f[:])
+                    nc.scalar.copy(out=q_grouped_w[:, c, :, :], in_=xt[:].rearrange("p u b -> p b u"))
+                nc.vector.quantize_mx(
+                    out=q_codes[:].rearrange("p c b -> p (c b)").bitcast(FP8X4),
+                    scales=q_scales[:].rearrange("p c b -> p (c b)"),
+                    in_=q_grouped[:].rearrange("p c b t -> p (c b t)"),
                 )
-            nc.vector.tensor_copy(out=neg_c_rows[:], in_=c_ps[:])
 
-            q_grouped = grouped_pool.tile([P, H_PASSES, QUERIES, PACK], BF16, tag="g1", align_bytes=64)
-            q_grouped_w = q_grouped[:].bitcast(F32)
-            for c in range(H_PASSES):
-                xt = ps_xt.tile([P, 2, QUERIES], F32, tag="xt")
-                for u in range(2):
-                    for t in range(Q_TILES):
-                        w0 = (2 * c + u) * P
-                        nc.tensor.transpose(xt[:, u, t * P : (t + 1) * P], q_words[:, t, w0 : w0 + P], ident_f[:])
-                nc.scalar.copy(out=q_grouped_w[:, c, :, :], in_=xt[:].rearrange("p u b -> p b u"))
-            nc.vector.quantize_mx(
-                out=q_codes[:].rearrange("p c b -> p (c b)").bitcast(FP8X4),
-                scales=q_scales[:].rearrange("p c b -> p (c b)"),
-                in_=q_grouped[:].rearrange("p c b t -> p (c b t)"),
-            )
+            def query_norms():
+                q_sq = stats.tile([P, Q_TILES], F32)
+                for t in range(Q_TILES):
+                    junk = work.tile([P, HID], BF16, tag="junk")
+                    nc.scalar.activation(out=junk[:], in_=q_raw[:, t, :], func=ACT.Square, accum_out=q_sq[:, t : t + 1])
+                q_recip = reciprocal_norm(nc, stats, q_sq[:], minus_half[:, 0:Q_TILES], Q_TILES)
+                nc.vector.tensor_scalar_mul(out=x_scale[:], in0=q_recip[:], scalar1=float(beta))
+                nc.vector.tensor_scalar_mul(out=neg_c[:], in0=q_recip[:], scalar1=-EPS)
+                c_ps = ps_st.tile([P, QUERIES], F32, tag="st")
+                for t in range(Q_TILES):
+                    nc.tensor.matmul(
+                        out=c_ps[:, t * P : (t + 1) * P],
+                        lhsT=neg_c[:, t : t + 1].to_broadcast([P, P]),
+                        rhs=ident_f[:],
+                        start=True,
+                        stop=True,
+                    )
+                nc.vector.tensor_copy(out=neg_c_rows[:], in_=c_ps[:])
 
+            e_sq = {}
+            gram = {}
             e_norm = {}
             g1 = {}
             st = {}
             g_t = {}
             y_n = {}
 
+            def gram_tiles(g):
+                return (2, 3) if g % 2 else (3,)
+
             def norms(g):
-                e_sq = stats.tile([P, PACK], F32)
+                e_sq[g] = stats.tile([P, PACK], F32, name="e_sq")
                 for j in range(PACK):
+                    if j in gram_tiles(g):
+                        continue
                     junk = work.tile([P, HID], BF16, tag="junk")
-                    nc.scalar.activation(out=junk[:], in_=e_raw[g][:, j, :], func=ACT.Square, accum_out=e_sq[:, j : j + 1])
-                e_norm[g] = (e_sq, rough_reciprocal_norm(nc, stats, e_sq[:], PACK))
+                    nc.scalar.activation(out=junk[:], in_=e_raw[g][:, j, :], func=ACT.Square, accum_out=e_sq[g][:, j : j + 1])
+
+            def gram_products(g):
+                gram[g] = ps_gram.tile([P, 2, P], F32, name="gram")
+                for s, j in enumerate(gram_tiles(g)):
+                    for c in range(H_PASSES):
+                        for t in range(PACK):
+                            part = g1[g][c][:, j * P : (j + 1) * P, t]
+                            nc.tensor.matmul(
+                                out=gram[g][:, s, :],
+                                lhsT=part,
+                                rhs=part,
+                                start=(c == 0 and t == 0),
+                                stop=(c == H_PASSES - 1 and t == PACK - 1),
+                            )
+
+            def gram_diagonals(g):
+                for s, j in enumerate(gram_tiles(g)):
+                    diagonal = work.tile([P, P], BF16)
+                    nc.vector.scalar_tensor_tensor(
+                        out=diagonal[:],
+                        in0=gram[g][:, s, :],
+                        scalar=1.0,
+                        in1=ident_f[:],
+                        op0=ALU.mult,
+                        op1=ALU.mult,
+                        accum_out=e_sq[g][:, j : j + 1],
+                    )
+                e_recip = reciprocal_norm(nc, stats, e_sq[g][:], minus_half[:], PACK)
+                e_recip_sq = stats.tile([P, PACK], F32)
+                nc.gpsimd.tensor_tensor(out=e_recip_sq[:], in0=e_recip[:], in1=e_recip[:], op=ALU.mult)
+                e_norm[g] = (e_recip, e_recip_sq)
 
             def transpose_words(g):
                 e_words = e_raw[g][:].bitcast(F32)
@@ -157,8 +197,7 @@ def tile_frozenhopfield_pa_kernel(tc, q, word_embs, beta, out):
                                 nc.tensor.transpose(
                                     xt[:, u, jj * P : (jj + 1) * P], e_words[:, 2 * jp + jj, w0 : w0 + P], ident_f[:]
                                 )
-                        copy_out = nc.vector.tensor_copy if (c, jp) == (H_PASSES - 1, 1) else nc.scalar.copy
-                        copy_out(out=grouped_w[:, jp * 2 * P : (jp + 1) * 2 * P, :], in_=xt[:].rearrange("p u v -> p v u"))
+                        nc.scalar.copy(out=grouped_w[:, jp * 2 * P : (jp + 1) * 2 * P, :], in_=xt[:].rearrange("p u v -> p v u"))
                     g1[g].append(grouped)
 
             def first_matmul(g):
@@ -170,20 +209,21 @@ def tile_frozenhopfield_pa_kernel(tc, q, word_embs, beta, out):
                         scales=e1_scales[:, c, :],
                         in_=g1[g][c][:].rearrange("p v t -> p (v t)"),
                     )
-                e_sq, guess = e_norm[g]
-                e_recip = newton_step(nc, stats, e_sq[:], guess, PACK)
-                e_recip_sq = stats.tile([P, PACK], F32)
-                nc.vector.tensor_mul(out=e_recip_sq[:], in0=e_recip[:], in1=e_recip[:])
+                first_products(g, e1_codes, e1_scales)
+
+            def scale_rows(g):
+                e_recip, e_recip_sq = e_norm[g]
                 g_t[g] = work.tile([P, PACK, QUERIES], F32, name="g_t")
                 for j in range(PACK):
-                    nc.vector.tensor_scalar(
+                    nc.scalar.activation(
                         out=g_t[g][:, j, :],
-                        in0=neg_c_rows[:],
-                        scalar1=e_recip_sq[:, j : j + 1],
-                        scalar2=e_recip[:, j : j + 1],
-                        op0=ALU.mult,
-                        op1=ALU.add,
+                        in_=neg_c_rows[:],
+                        func=ACT.Identity,
+                        scale=e_recip_sq[:, j : j + 1],
+                        bias=e_recip[:, j : j + 1],
                     )
+
+            def first_products(g, e1_codes, e1_scales):
                 st[g] = []
                 for jp in range(PACK // 2):
                     s_t = ps_st.tile([P, 2, QUERIES], F32, tag="st")
@@ -217,8 +257,8 @@ def tile_frozenhopfield_pa_kernel(tc, q, word_embs, beta, out):
             def keep_and_max(g):
                 for t in range(Q_TILES):
                     nc.vector.tensor_scalar(
-                        out=x_sb[:, t, g * K_PASS : (g + 1) * K_PASS],
-                        in0=y_n[g][t][:],
+                        out=x_sb[:, t, g * K_PASS : (g + 1) * K_PASS].rearrange("p (u w e) -> p u w e", u=2, e=2),
+                        in0=y_n[g][t][:].rearrange("p (u e w) -> p u w e", u=2, e=2),
                         scalar1=x_scale[:, t : t + 1],
                         scalar2=None,
                         op0=ALU.mult,
@@ -227,21 +267,36 @@ def tile_frozenhopfield_pa_kernel(tc, q, word_embs, beta, out):
                     )
 
             load(0)
+            nc.sync.dma_start(out=q_raw[:], in_=q.rearrange("(t p) h -> p t h", p=P))
             load(1)
-            for i in range(-2, GROUPS):
+            load(2)
+            transpose_words(0)
+            quantise_queries()
+            norms(0)
+            query_norms()
+            regroup_for_second_matmul(0)
+            quantise_for_second_matmul(0)
+            for i in range(-1, GROUPS):
                 if i + 4 < GROUPS:
                     load(i + 4)
+                if 0 <= i + 1 < GROUPS:
+                    gram_products(i + 1)
                 if i >= 0:
                     normalise_and_turn(i)
                 if 0 <= i + 1 < GROUPS:
+                    gram_diagonals(i + 1)
                     first_matmul(i + 1)
                 if i + 2 < GROUPS:
-                    norms(i + 2)
                     transpose_words(i + 2)
+                    norms(i + 2)
                     if i + 2 < GROUPS - LATE:
                         regroup_for_second_matmul(i + 2)
                 if i >= 0:
                     keep_and_max(i)
+                if i + 2 < GROUPS - LATE:
+                    quantise_for_second_matmul(i + 2)
+                if 0 <= i + 1 < GROUPS:
+                    scale_rows(i + 1)
 
         with (
             tc.tile_pool(name="late", bufs=1) as late,
@@ -278,13 +333,16 @@ def tile_frozenhopfield_pa_kernel(tc, q, word_embs, beta, out):
             def turn_and_quantise(u):
                 p_grouped = turned_pool.tile([P, PAIR, QUERIES, PACK], BF16, align_bytes=64)
                 for gl in range(PAIR):
-                    p_t = ps_pt.tile([P, PACK, QUERIES], BF16, tag="pt")
-                    for j in range(PACK):
+                    p_t = ps_pt.tile([P, 2, QUERIES], F32, tag="pt")
+                    for half in range(2):
                         for t in range(Q_TILES):
-                            v0 = (gl * PACK + j) * P
-                            nc.tensor.transpose(p_t[:, j, t * P : (t + 1) * P], p_bf[(u, t)][:, v0 : v0 + P], ident_b[:])
-                    copy_out = nc.vector.tensor_copy if gl == 0 else nc.scalar.copy
-                    copy_out(out=p_grouped[:, gl, :, :], in_=p_t[:].rearrange("p j b -> p b j"))
+                            w0 = (gl * 2 + half) * P
+                            p_words = p_bf[(u, t)][:].bitcast(F32)
+                            nc.tensor.transpose(p_t[:, half, t * P : (t + 1) * P], p_words[:, w0 : w0 + P], ident_f[:])
+                    nc.scalar.copy(
+                        out=p_grouped[:, gl, :, :].rearrange("p b t -> p (b t)").bitcast(F32).rearrange("p (b k) -> p b k", k=2),
+                        in_=p_t[:].rearrange("p k b -> p b k"),
+                    )
                 nc.vector.quantize_mx(
                     out=p_codes[:, u * PAIR : (u + 1) * PAIR, :].rearrange("p g b -> p (g b)").bitcast(FP8X4),
                     scales=p_scales[:, u * PAIR : (u + 1) * PAIR, :].rearrange("p g b -> p (g b)"),
@@ -312,10 +370,12 @@ def tile_frozenhopfield_pa_kernel(tc, q, word_embs, beta, out):
             for u in range(units + 1):
                 if u + 1 < units:
                     exponentials(u + 1)
+                if u < LATE:
+                    regroup_for_second_matmul(GROUPS - LATE + u)
                 if u < units:
                     turn_and_quantise(u)
                 if u < LATE:
-                    regroup_for_second_matmul(GROUPS - LATE + u)
+                    quantise_for_second_matmul(GROUPS - LATE + u)
                     if u + 3 < LATE:
                         load(GROUPS - LATE + u + 3)
                 if u >= 1:

@@ -30,11 +30,18 @@ TINY = 1e-30
 LATE = 6
 
 
-def reciprocal_norm(nc, pool, sum_sq, minus_half, width):
-    shifted = pool.tile([P, width], F32)
-    nc.gpsimd.tensor_scalar(out=shifted[:], in0=sum_sq, scalar1=1.0, scalar2=TINY, op0=ALU.mult, op1=ALU.add)
+def rough_reciprocal_norm(nc, pool, sum_sq, width):
+    guess = pool.tile([P, width], F32)
+    nc.scalar.activation(out=guess[:], in_=sum_sq, func=ACT.Abs_reciprocal_sqrt, bias=TINY)
+    return guess
+
+
+def newton_step(nc, pool, sum_sq, guess, width):
+    factor = pool.tile([P, width], F32)
+    nc.vector.scalar_tensor_tensor(out=factor[:], in0=guess[:], scalar=-0.5, in1=guess[:], op0=ALU.mult, op1=ALU.mult)
+    nc.vector.tensor_mul(out=factor[:], in0=factor[:], in1=sum_sq)
     recip = pool.tile([P, width], F32)
-    nc.gpsimd.tensor_tensor(out=recip[:], in0=shifted[:], in1=minus_half, op=ALU.pow)
+    nc.vector.scalar_tensor_tensor(out=recip[:], in0=factor[:], scalar=1.5, in1=guess[:], op0=ALU.add, op1=ALU.mult)
     return recip
 
 
@@ -43,9 +50,6 @@ def tile_frozenhopfield_pa_kernel(tc, q, word_embs, beta, out):
     with tc.tile_pool(name="keep", bufs=1) as keep, tc.tile_pool(name="stream", bufs=3) as stream:
         ident_f = keep.tile([P, P], F32)
         make_identity(nc, ident_f[:])
-
-        minus_half = keep.tile([P, PACK], F32)
-        nc.gpsimd.memset(minus_half[:], -0.5)
 
         x_sb = keep.tile([P, Q_TILES, VOCAB], F32)
         e2_codes = keep.tile([P, GROUPS, HID], U32, align_bytes=64)
@@ -119,7 +123,8 @@ def tile_frozenhopfield_pa_kernel(tc, q, word_embs, beta, out):
                 for t in range(Q_TILES):
                     junk = work.tile([P, HID], BF16, tag="junk")
                     nc.scalar.activation(out=junk[:], in_=q_raw[:, t, :], func=ACT.Square, accum_out=q_sq[:, t : t + 1])
-                q_recip = reciprocal_norm(nc, stats, q_sq[:], minus_half[:, 0:Q_TILES], Q_TILES)
+                q_guess = rough_reciprocal_norm(nc, stats, q_sq[:], Q_TILES)
+                q_recip = newton_step(nc, stats, q_sq[:], q_guess, Q_TILES)
                 nc.vector.tensor_scalar_mul(out=x_scale[:], in0=q_recip[:], scalar1=float(beta))
                 nc.vector.tensor_scalar_mul(out=neg_c[:], in0=q_recip[:], scalar1=-EPS)
                 c_ps = ps_st.tile([P, QUERIES], F32, tag="st")
@@ -178,10 +183,7 @@ def tile_frozenhopfield_pa_kernel(tc, q, word_embs, beta, out):
                         op1=ALU.mult,
                         accum_out=e_sq[g][:, j : j + 1],
                     )
-                e_recip = reciprocal_norm(nc, stats, e_sq[g][:], minus_half[:], PACK)
-                e_recip_sq = stats.tile([P, PACK], F32)
-                nc.gpsimd.tensor_tensor(out=e_recip_sq[:], in0=e_recip[:], in1=e_recip[:], op=ALU.mult)
-                e_norm[g] = (e_recip, e_recip_sq)
+                e_norm[g] = rough_reciprocal_norm(nc, stats, e_sq[g][:], PACK)
 
             def transpose_words(g):
                 e_words = e_raw[g][:].bitcast(F32)
@@ -212,7 +214,9 @@ def tile_frozenhopfield_pa_kernel(tc, q, word_embs, beta, out):
                 first_products(g, e1_codes, e1_scales)
 
             def scale_rows(g):
-                e_recip, e_recip_sq = e_norm[g]
+                e_recip = newton_step(nc, stats, e_sq[g][:], e_norm[g], PACK)
+                e_recip_sq = stats.tile([P, PACK], F32)
+                nc.vector.tensor_mul(out=e_recip_sq[:], in0=e_recip[:], in1=e_recip[:])
                 g_t[g] = work.tile([P, PACK, QUERIES], F32, name="g_t")
                 for j in range(PACK):
                     nc.scalar.activation(

@@ -97,7 +97,6 @@ def tile_frozenhopfield_pa_kernel(tc, q, word_embs, beta, out):
             tc.psum_pool(name="ps_xt", bufs=3) as ps_xt,
             tc.psum_pool(name="ps_st", bufs=2) as ps_st,
             tc.psum_pool(name="ps_yn", bufs=2) as ps_yn,
-            tc.psum_pool(name="ps_gram", bufs=1) as ps_gram,
         ):
             q_raw = work.tile([P, Q_TILES, HID], BF16, tag="y_t")
 
@@ -139,53 +138,17 @@ def tile_frozenhopfield_pa_kernel(tc, q, word_embs, beta, out):
                 nc.vector.tensor_copy(out=neg_c_rows[:], in_=c_ps[:])
 
             e_sq = {}
-            gram = {}
-            e_norm = {}
+            guess = {}
+            recip = {}
+            recip_sq = {}
             g1 = {}
+            e1 = {}
             st = {}
             g_t = {}
+            y_t = {}
             y_n = {}
 
-            def gram_tiles(g):
-                return (2, 3) if g % 2 else (3,)
-
-            def norms(g):
-                e_sq[g] = stats.tile([P, PACK], F32, name="e_sq")
-                for j in range(PACK):
-                    if j in gram_tiles(g):
-                        continue
-                    junk = work.tile([P, HID], BF16, tag="junk")
-                    nc.scalar.activation(out=junk[:], in_=e_raw[g][:, j, :], func=ACT.Square, accum_out=e_sq[g][:, j : j + 1])
-
-            def gram_products(g):
-                gram[g] = ps_gram.tile([P, 2, P], F32, name="gram")
-                for s, j in enumerate(gram_tiles(g)):
-                    for c in range(H_PASSES):
-                        for t in range(PACK):
-                            part = g1[g][c][:, j * P : (j + 1) * P, t]
-                            nc.tensor.matmul(
-                                out=gram[g][:, s, :],
-                                lhsT=part,
-                                rhs=part,
-                                start=(c == 0 and t == 0),
-                                stop=(c == H_PASSES - 1 and t == PACK - 1),
-                            )
-
-            def gram_diagonals(g):
-                for s, j in enumerate(gram_tiles(g)):
-                    diagonal = work.tile([P, P], BF16)
-                    nc.vector.scalar_tensor_tensor(
-                        out=diagonal[:],
-                        in0=gram[g][:, s, :],
-                        scalar=1.0,
-                        in1=ident_f[:],
-                        op0=ALU.mult,
-                        op1=ALU.mult,
-                        accum_out=e_sq[g][:, j : j + 1],
-                    )
-                e_norm[g] = rough_reciprocal_norm(nc, stats, e_sq[g][:], PACK)
-
-            def transpose_words(g):
+            def turn_words(g):
                 e_words = e_raw[g][:].bitcast(F32)
                 g1[g] = []
                 for c in range(H_PASSES):
@@ -202,32 +165,42 @@ def tile_frozenhopfield_pa_kernel(tc, q, word_embs, beta, out):
                         nc.scalar.copy(out=grouped_w[:, jp * 2 * P : (jp + 1) * 2 * P, :], in_=xt[:].rearrange("p u v -> p v u"))
                     g1[g].append(grouped)
 
-            def first_matmul(g):
-                e1_codes = work.tile([P, H_PASSES, K_PASS], U32, align_bytes=64)
-                e1_scales = work.tile([P, H_PASSES, K_PASS], U8, align_bytes=64)
-                for c in range(H_PASSES):
-                    nc.vector.quantize_mx(
-                        out=e1_codes[:, c, :].bitcast(FP8X4),
-                        scales=e1_scales[:, c, :],
-                        in_=g1[g][c][:].rearrange("p v t -> p (v t)"),
-                    )
-                first_products(g, e1_codes, e1_scales)
-
-            def scale_rows(g):
-                e_recip = newton_step(nc, stats, e_sq[g][:], e_norm[g], PACK)
-                e_recip_sq = stats.tile([P, PACK], F32)
-                nc.vector.tensor_mul(out=e_recip_sq[:], in0=e_recip[:], in1=e_recip[:])
-                g_t[g] = work.tile([P, PACK, QUERIES], F32, name="g_t")
+            def squared_norms(g):
+                e_sq[g] = stats.tile([P, PACK], F32, name="e_sq")
                 for j in range(PACK):
-                    nc.scalar.activation(
-                        out=g_t[g][:, j, :],
-                        in_=neg_c_rows[:],
-                        func=ACT.Identity,
-                        scale=e_recip_sq[:, j : j + 1],
-                        bias=e_recip[:, j : j + 1],
-                    )
+                    junk = work.tile([P, HID], BF16, tag="junk")
+                    nc.scalar.activation(out=junk[:], in_=e_raw[g][:, j, :], func=ACT.Square, accum_out=e_sq[g][:, j : j + 1])
+                guess[g] = rough_reciprocal_norm(nc, stats, e_sq[g][:], PACK)
 
-            def first_products(g, e1_codes, e1_scales):
+            def newton_steps(g):
+                factor = stats.tile([P, PACK], F32)
+                recip[g] = stats.tile([P, PACK], F32, name="recip")
+                recip_sq[g] = stats.tile([P, PACK], F32, name="recip_sq")
+                return [
+                    lambda: nc.vector.scalar_tensor_tensor(
+                        out=factor[:], in0=guess[g][:], scalar=-0.5, in1=guess[g][:], op0=ALU.mult, op1=ALU.mult
+                    ),
+                    lambda: nc.vector.tensor_mul(out=factor[:], in0=factor[:], in1=e_sq[g][:]),
+                    lambda: nc.vector.scalar_tensor_tensor(
+                        out=recip[g][:], in0=factor[:], scalar=1.5, in1=guess[g][:], op0=ALU.add, op1=ALU.mult
+                    ),
+                    lambda: nc.vector.tensor_mul(out=recip_sq[g][:], in0=recip[g][:], in1=recip[g][:]),
+                ]
+
+            def quantise_words(g, c):
+                if c == 0:
+                    codes = work.tile([P, H_PASSES, K_PASS], U32, name="e1_codes", align_bytes=64)
+                    scales = work.tile([P, H_PASSES, K_PASS], U8, name="e1_scales", align_bytes=64)
+                    e1[g] = (codes, scales)
+                codes, scales = e1[g]
+                nc.vector.quantize_mx(
+                    out=codes[:, c, :].bitcast(FP8X4),
+                    scales=scales[:, c, :],
+                    in_=g1[g][c][:].rearrange("p v t -> p (v t)"),
+                )
+
+            def first_products(g):
+                codes, scales = e1[g]
                 st[g] = []
                 for jp in range(PACK // 2):
                     s_t = ps_st.tile([P, 2, QUERIES], F32, tag="st")
@@ -236,8 +209,8 @@ def tile_frozenhopfield_pa_kernel(tc, q, word_embs, beta, out):
                         for c in range(H_PASSES):
                             nc.tensor.matmul_mx(
                                 out=s_t[:, jj, :],
-                                lhsT=e1_codes[:, c, j * P : (j + 1) * P].bitcast(FP8X4),
-                                lhsT_scale=e1_scales[:, c, j * P : (j + 1) * P],
+                                lhsT=codes[:, c, j * P : (j + 1) * P].bitcast(FP8X4),
+                                lhsT_scale=scales[:, c, j * P : (j + 1) * P],
                                 rhs=q_codes[:, c, :].bitcast(FP8X4),
                                 rhs_scale=q_scales[:, c, :],
                                 start=(c == 0),
@@ -245,62 +218,85 @@ def tile_frozenhopfield_pa_kernel(tc, q, word_embs, beta, out):
                             )
                     st[g].append(s_t)
 
-            def normalise_and_turn(g):
-                y_t = work.tile([P, PACK, QUERIES], F32)
-                for jp in range(PACK // 2):
-                    nc.vector.tensor_tensor(
-                        out=y_t[:, 2 * jp : 2 * jp + 2, :], in0=st[g][jp][:], in1=g_t[g][:, 2 * jp : 2 * jp + 2, :], op=ALU.mult
+            def scale_rows(g):
+                g_t[g] = work.tile([P, PACK, QUERIES], F32, name="g_t")
+                for j in range(PACK):
+                    nc.vector.tensor_scalar(
+                        out=g_t[g][:, j, :],
+                        in0=neg_c_rows[:],
+                        scalar1=recip_sq[g][:, j : j + 1],
+                        scalar2=recip[g][:, j : j + 1],
+                        op0=ALU.mult,
+                        op1=ALU.add,
                     )
+
+            def normalise(g, jp):
+                if jp == 0:
+                    y_t[g] = work.tile([P, PACK, QUERIES], F32, name="y_t")
+                js = slice(2 * jp, 2 * jp + 2)
+                nc.vector.tensor_tensor(out=y_t[g][:, js, :], in0=st[g][jp][:], in1=g_t[g][:, js, :], op=ALU.mult)
+
+            def turn_scores(g):
                 y_n[g] = []
                 for t in range(Q_TILES):
                     turned = ps_yn.tile([P, BANK], F32, tag="yn")
                     for j in range(PACK):
-                        nc.tensor.transpose(turned[:, j * P : (j + 1) * P], y_t[:, j, t * P : (t + 1) * P], ident_f[:])
+                        nc.tensor.transpose(turned[:, j * P : (j + 1) * P], y_t[g][:, j, t * P : (t + 1) * P], ident_f[:])
                     y_n[g].append(turned)
 
-            def keep_and_max(g):
-                for t in range(Q_TILES):
-                    nc.vector.tensor_scalar(
-                        out=x_sb[:, t, g * K_PASS : (g + 1) * K_PASS].rearrange("p (u w e) -> p u w e", u=2, e=2),
-                        in0=y_n[g][t][:].rearrange("p (u e w) -> p u w e", u=2, e=2),
-                        scalar1=x_scale[:, t : t + 1],
-                        scalar2=None,
-                        op0=ALU.mult,
-                        op1=ALU.max,
-                        accum_out=part_max[:, t, g : g + 1],
-                    )
+            def keep_and_max(g, t):
+                nc.vector.tensor_scalar(
+                    out=x_sb[:, t, g * K_PASS : (g + 1) * K_PASS].rearrange("p (u w e) -> p u w e", u=2, e=2),
+                    in0=y_n[g][t][:].rearrange("p (u e w) -> p u w e", u=2, e=2),
+                    scalar1=x_scale[:, t : t + 1],
+                    scalar2=None,
+                    op0=ALU.mult,
+                    op1=ALU.max,
+                    accum_out=part_max[:, t, g : g + 1],
+                )
 
             load(0)
             nc.sync.dma_start(out=q_raw[:], in_=q.rearrange("(t p) h -> p t h", p=P))
             load(1)
             load(2)
-            transpose_words(0)
+            turn_words(0)
             quantise_queries()
-            norms(0)
+            squared_norms(0)
             query_norms()
             regroup_for_second_matmul(0)
             quantise_for_second_matmul(0)
-            for i in range(-1, GROUPS):
-                if i + 4 < GROUPS:
-                    load(i + 4)
-                if 0 <= i + 1 < GROUPS:
-                    gram_products(i + 1)
-                if i >= 0:
-                    normalise_and_turn(i)
-                if 0 <= i + 1 < GROUPS:
-                    gram_diagonals(i + 1)
-                    first_matmul(i + 1)
-                if i + 2 < GROUPS:
-                    transpose_words(i + 2)
-                    norms(i + 2)
+            with tc.manual_schedule(engines={mybir.EngineType.DVE}):
+                for i in range(-1, GROUPS):
+                    now = i >= 0
+                    ahead = i + 1 < GROUPS
+                    fresh = i + 2 < GROUPS
+                    if i + 4 < GROUPS:
+                        load(i + 4)
+                    if fresh:
+                        turn_words(i + 2)
+                        squared_norms(i + 2)
+                    newton = newton_steps(i + 1) if ahead else []
+                    for step in range(2):
+                        if ahead:
+                            newton[step]()
+                        if now:
+                            normalise(i, step)
+                    if now:
+                        turn_scores(i)
+                    if ahead:
+                        for c in range(H_PASSES):
+                            newton[2 + c]()
+                            quantise_words(i + 1, c)
+                        first_products(i + 1)
                     if i + 2 < GROUPS - LATE:
                         regroup_for_second_matmul(i + 2)
-                if i >= 0:
-                    keep_and_max(i)
-                if i + 2 < GROUPS - LATE:
-                    quantise_for_second_matmul(i + 2)
-                if 0 <= i + 1 < GROUPS:
-                    scale_rows(i + 1)
+                    if now:
+                        for t in range(Q_TILES):
+                            keep_and_max(i, t)
+                    if i + 2 < GROUPS - LATE:
+                        quantise_for_second_matmul(i + 2)
+                    if ahead:
+                        scale_rows(i + 1)
 
         with (
             tc.tile_pool(name="late", bufs=1) as late,
@@ -343,7 +339,8 @@ def tile_frozenhopfield_pa_kernel(tc, q, word_embs, beta, out):
                             w0 = (gl * 2 + half) * P
                             p_words = p_bf[(u, t)][:].bitcast(F32)
                             nc.tensor.transpose(p_t[:, half, t * P : (t + 1) * P], p_words[:, w0 : w0 + P], ident_f[:])
-                    nc.scalar.copy(
+                    copy_out = nc.vector.tensor_copy if gl == 0 else nc.scalar.copy
+                    copy_out(
                         out=p_grouped[:, gl, :, :].rearrange("p b t -> p (b t)").bitcast(F32).rearrange("p (b k) -> p b k", k=2),
                         in_=p_t[:].rearrange("p k b -> p b k"),
                     )

@@ -25,29 +25,20 @@ H_PASSES = HID // K_PASS
 GROUPS = VOCAB // K_PASS
 H_HALVES = HID // BANK
 PAIR = 2
+UNITS = GROUPS // PAIR
 EPS = 1e-8
 TINY = 1e-30
-LATE = 6
-
-
-def rough_reciprocal_norm(nc, pool, sum_sq, width):
-    guess = pool.tile([P, width], F32)
-    nc.scalar.activation(out=guess[:], in_=sum_sq, func=ACT.Abs_reciprocal_sqrt, bias=TINY)
-    return guess
-
-
-def newton_step(nc, pool, sum_sq, guess, width):
-    factor = pool.tile([P, width], F32)
-    nc.vector.scalar_tensor_tensor(out=factor[:], in0=guess[:], scalar=-0.5, in1=guess[:], op0=ALU.mult, op1=ALU.mult)
-    nc.vector.tensor_mul(out=factor[:], in0=factor[:], in1=sum_sq)
-    recip = pool.tile([P, width], F32)
-    nc.vector.scalar_tensor_tensor(out=recip[:], in0=factor[:], scalar=1.5, in1=guess[:], op0=ALU.add, op1=ALU.mult)
-    return recip
+GRAM = (3,)
+ROWS_ON_SCALAR = 2
+LATE = (4, 7, 10, 13)
+LAST = (14, 15)
 
 
 def tile_frozenhopfield_pa_kernel(tc, q, word_embs, beta, out):
     nc = tc.nc
-    with tc.tile_pool(name="keep", bufs=1) as keep, tc.tile_pool(name="stream", bufs=3) as stream:
+    with tc.tile_pool(name="keep", bufs=1) as keep, tc.tile_pool(name="stream", bufs=3) as stream, tc.tile_pool(
+        name="regroup", bufs=2
+    ) as regroup_pool, tc.tile_pool(name="stats", bufs=3) as stats:
         ident_f = keep.tile([P, P], F32)
         make_identity(nc, ident_f[:])
 
@@ -60,73 +51,248 @@ def tile_frozenhopfield_pa_kernel(tc, q, word_embs, beta, out):
         x_scale = keep.tile([P, Q_TILES], F32)
         neg_c = keep.tile([P, Q_TILES], F32)
         part_max = keep.tile([P, Q_TILES, GROUPS], F32)
-        part_sum = keep.tile([P, Q_TILES, GROUPS // PAIR], F32)
+        part_sum = keep.tile([P, Q_TILES, UNITS], F32)
 
         e_raw = {}
         regrouped = {}
 
-        def load(g):
+        def load(g, pieces=1):
             e_raw[g] = stream.tile([P, PACK, HID], BF16, name="e_raw")
-            rows = word_embs[g * K_PASS : (g + 1) * K_PASS, :]
-            nc.sync.dma_start(out=e_raw[g][:], in_=rows.rearrange("(p j) h -> p j h", j=PACK))
+            rows = word_embs[g * K_PASS : (g + 1) * K_PASS, :].rearrange("(p j) h -> p j h", j=PACK)
+            n = PACK // pieces
+            for k in range(pieces):
+                nc.sync.dma_start(out=e_raw[g][:, k * n : (k + 1) * n, :], in_=rows[:, k * n : (k + 1) * n, :])
 
-        def regroup_for_second_matmul(g):
-            regrouped[g] = []
-            for hh in range(H_HALVES):
-                cols = slice(hh * BANK, (hh + 1) * BANK)
-                g2 = stream.tile([P, BANK, PACK], BF16, align_bytes=64)
-                nc.vector.tensor_copy(
-                    out=g2[:].rearrange("p (c i) t -> p c t i", i=4),
-                    in_=e_raw[g][:, :, cols].rearrange("p t (c i) -> p c t i", i=4),
-                )
-                regrouped[g].append(g2)
+        def regroup(g, lo=0, hi=HID):
+            if lo == 0:
+                regrouped[g] = regroup_pool.tile([P, HID, PACK], BF16, name="e_regrouped", align_bytes=64)
+            nc.vector.tensor_copy(
+                out=regrouped[g][:, lo:hi, :].rearrange("p (c i) t -> p c t i", i=4),
+                in_=e_raw[g][:, :, lo:hi].rearrange("p t (c i) -> p c t i", i=4),
+            )
 
-        def quantise_for_second_matmul(g):
-            for hh in range(H_HALVES):
-                cols = slice(hh * BANK, (hh + 1) * BANK)
-                nc.vector.quantize_mx(
-                    out=e2_codes[:, g, cols].bitcast(FP8X4),
-                    scales=e2_scales[:, g, cols],
-                    in_=regrouped[g][hh][:].rearrange("p h t -> p (h t)"),
-                )
+        def quantise_regrouped(g, lo=0, hi=HID):
+            nc.vector.quantize_mx(
+                out=e2_codes[:, g, lo:hi].bitcast(FP8X4),
+                scales=e2_scales[:, g, lo:hi],
+                in_=regrouped[g][:, lo:hi, :].rearrange("p h t -> p (h t)"),
+            )
 
-        with (
-            tc.tile_pool(name="grouped", bufs=4) as grouped_pool,
-            tc.tile_pool(name="work", bufs=2) as work,
-            tc.tile_pool(name="stats", bufs=3) as stats,
-            tc.psum_pool(name="ps_xt", bufs=3) as ps_xt,
-            tc.psum_pool(name="ps_st", bufs=2) as ps_st,
-            tc.psum_pool(name="ps_yn", bufs=2) as ps_yn,
-        ):
-            q_raw = work.tile([P, Q_TILES, HID], BF16, tag="y_t")
+        def rough_reciprocal_norm(sum_sq, width):
+            rough = stats.tile([P, width], F32)
+            nc.scalar.activation(out=rough[:], in_=sum_sq, func=ACT.Abs_reciprocal_sqrt, bias=TINY)
+            return rough
 
-            def quantise_queries():
+        def newton_steps(sum_sq, rough, width):
+            factor = stats.tile([P, width], F32)
+            recip = stats.tile([P, width], F32)
+            recip_sq = stats.tile([P, width], F32)
+            calls = [
+                lambda: nc.vector.scalar_tensor_tensor(
+                    out=factor[:], in0=rough[:], scalar=-0.5, in1=rough[:], op0=ALU.mult, op1=ALU.mult
+                ),
+                lambda: nc.vector.tensor_mul(out=factor[:], in0=factor[:], in1=sum_sq),
+                lambda: nc.vector.scalar_tensor_tensor(
+                    out=recip[:], in0=factor[:], scalar=1.5, in1=rough[:], op0=ALU.add, op1=ALU.mult
+                ),
+                lambda: nc.vector.tensor_mul(out=recip_sq[:], in0=recip[:], in1=recip[:]),
+            ]
+            return calls, recip, recip_sq
+
+        with tc.manual_schedule():
+            with (
+                tc.tile_pool(name="work", bufs=2) as work,
+                tc.psum_pool(name="ps_xt", bufs=4) as ps_xt,
+                tc.psum_pool(name="ps_st", bufs=2) as ps_st,
+                tc.psum_pool(name="ps_yn", bufs=2) as ps_yn,
+            ):
+                e_sq = {}
+                gram = {}
+                rough = {}
+                recip = {}
+                g1 = {}
+                e1 = {}
+                st = {}
+                g_t = {}
+                y_t = {}
+                y_n = {}
+
+                def turn_words(g):
+                    e_words = e_raw[g][:].bitcast(F32)
+                    g1[g] = work.tile([P, H_PASSES, K_PASS, PACK], BF16, name="g1", align_bytes=64)
+                    for c in range(H_PASSES):
+                        grouped_w = g1[g][:].bitcast(F32)[:, c, :, :]
+                        for jp in range(PACK // 2):
+                            xt = ps_xt.tile([P, 2, 2 * P], F32, tag="xt")
+                            for u in range(2):
+                                for jj in range(2):
+                                    w0 = (2 * c + u) * P
+                                    nc.tensor.transpose(
+                                        xt[:, u, jj * P : (jj + 1) * P], e_words[:, 2 * jp + jj, w0 : w0 + P], ident_f[:]
+                                    )
+                            nc.scalar.copy(
+                                out=grouped_w[:, jp * 2 * P : (jp + 1) * 2 * P, :], in_=xt[:].rearrange("p u v -> p v u")
+                            )
+
+                def gram_products(g):
+                    gram[g] = ps_xt.tile([P, len(GRAM), P], F32, name="gram", tag="xt")
+                    for k, j in enumerate(GRAM):
+                        for c in range(H_PASSES):
+                            for t in range(PACK):
+                                part = g1[g][:, c, j * P : (j + 1) * P, t]
+                                nc.tensor.matmul(
+                                    out=gram[g][:, k, :],
+                                    lhsT=part,
+                                    rhs=part,
+                                    start=(c == 0 and t == 0),
+                                    stop=(c == H_PASSES - 1 and t == PACK - 1),
+                                )
+
+                def gram_diagonals(g):
+                    for k, j in enumerate(GRAM):
+                        diagonal = work.tile([P, P], BF16)
+                        nc.vector.scalar_tensor_tensor(
+                            out=diagonal[:],
+                            in0=gram[g][:, k, :],
+                            scalar=1.0,
+                            in1=ident_f[:],
+                            op0=ALU.mult,
+                            op1=ALU.mult,
+                            accum_out=e_sq[g][:, j : j + 1],
+                        )
+
+                def squared_norms(g):
+                    e_sq[g] = stats.tile([P, PACK], F32, name="e_sq")
+                    for j in range(PACK):
+                        if j in GRAM:
+                            continue
+                        junk = work.tile([P, HID], BF16, tag="junk")
+                        nc.scalar.activation(
+                            out=junk[:], in_=e_raw[g][:, j, :], func=ACT.Square, accum_out=e_sq[g][:, j : j + 1]
+                        )
+
+                def quantise_words(g):
+                    codes = work.tile([P, H_PASSES, K_PASS], U32, name="e1_codes", align_bytes=64)
+                    scales = work.tile([P, H_PASSES, K_PASS], U8, name="e1_scales", align_bytes=64)
+                    e1[g] = (codes, scales)
+                    nc.vector.quantize_mx(
+                        out=codes[:].rearrange("p c v -> p (c v)").bitcast(FP8X4),
+                        scales=scales[:].rearrange("p c v -> p (c v)"),
+                        in_=g1[g][:].rearrange("p c v t -> p (c v t)"),
+                    )
+
+                def first_products(g):
+                    codes, scales = e1[g]
+                    st[g] = []
+                    for jp in range(PACK // 2):
+                        s_t = ps_st.tile([P, 2, QUERIES], F32, tag="st")
+                        for jj in range(2):
+                            j = 2 * jp + jj
+                            for c in range(H_PASSES):
+                                nc.tensor.matmul_mx(
+                                    out=s_t[:, jj, :],
+                                    lhsT=codes[:, c, j * P : (j + 1) * P].bitcast(FP8X4),
+                                    lhsT_scale=scales[:, c, j * P : (j + 1) * P],
+                                    rhs=q_codes[:, c, :].bitcast(FP8X4),
+                                    rhs_scale=q_scales[:, c, :],
+                                    start=(c == 0),
+                                    stop=(c == H_PASSES - 1),
+                                )
+                        st[g].append(s_t)
+
+                def scale_rows(g):
+                    r, r_sq = recip[g]
+                    g_t[g] = work.tile([P, PACK, QUERIES], F32, name="g_t", align_bytes=64)
+                    for j in range(ROWS_ON_SCALAR):
+                        nc.scalar.activation(
+                            out=g_t[g][:, j, :],
+                            in_=neg_c_rows[:],
+                            func=ACT.Identity,
+                            scale=r_sq[:, j : j + 1],
+                            bias=r[:, j : j + 1],
+                        )
+                    for j in range(ROWS_ON_SCALAR, PACK):
+                        nc.vector.tensor_scalar(
+                            out=g_t[g][:, j, :],
+                            in0=neg_c_rows[:],
+                            scalar1=r_sq[:, j : j + 1],
+                            scalar2=r[:, j : j + 1],
+                            op0=ALU.mult,
+                            op1=ALU.add,
+                        )
+
+                def normalise(g):
+                    y_t[g] = work.tile([P, PACK, QUERIES], F32, name="y_t")
+                    for jp in range(PACK // 2):
+                        js = slice(2 * jp, 2 * jp + 2)
+                        nc.vector.tensor_tensor(out=y_t[g][:, js, :], in0=st[g][jp][:], in1=g_t[g][:, js, :], op=ALU.mult)
+
+                def turn_scores(g):
+                    y_n[g] = []
+                    for t in range(Q_TILES):
+                        turned = ps_yn.tile([P, BANK], F32, tag="yn")
+                        for j in range(PACK):
+                            nc.tensor.transpose(turned[:, j * P : (j + 1) * P], y_t[g][:, j, t * P : (t + 1) * P], ident_f[:])
+                        y_n[g].append(turned)
+
+                def keep_and_max(g, t):
+                    nc.vector.tensor_scalar(
+                        out=x_sb[:, t, g * K_PASS : (g + 1) * K_PASS].rearrange("p (u w e) -> p u w e", u=2, e=2),
+                        in0=y_n[g][t][:].rearrange("p (u e w) -> p u w e", u=2, e=2),
+                        scalar1=x_scale[:, t : t + 1],
+                        scalar2=None,
+                        op0=ALU.mult,
+                        op1=ALU.max,
+                        accum_out=part_max[:, t, g : g + 1],
+                    )
+
+                load(0, pieces=PACK)
+                q_raw = work.tile([P, Q_TILES, HID], BF16, tag="y_t")
+                nc.sync.dma_start(out=q_raw[:], in_=q.rearrange("(t p) h -> p t h", p=P))
+                load(1)
+                load(2)
+
+                turn_words(0)
+                regroup(0)
+
                 q_words = q_raw[:].bitcast(F32)
-                q_grouped = grouped_pool.tile([P, H_PASSES, QUERIES, PACK], BF16, tag="g1", align_bytes=64)
-                q_grouped_w = q_grouped[:].bitcast(F32)
+                q_grouped = work.tile([P, H_PASSES, QUERIES, PACK], BF16, tag="g_t", align_bytes=64)
                 for c in range(H_PASSES):
                     xt = ps_xt.tile([P, 2, QUERIES], F32, tag="xt")
                     for u in range(2):
                         for t in range(Q_TILES):
                             w0 = (2 * c + u) * P
                             nc.tensor.transpose(xt[:, u, t * P : (t + 1) * P], q_words[:, t, w0 : w0 + P], ident_f[:])
-                    nc.scalar.copy(out=q_grouped_w[:, c, :, :], in_=xt[:].rearrange("p u b -> p b u"))
+                    nc.scalar.copy(out=q_grouped[:].bitcast(F32)[:, c, :, :], in_=xt[:].rearrange("p u b -> p b u"))
+
+                q_sq = stats.tile([P, Q_TILES], F32)
+                for t in range(Q_TILES):
+                    junk = work.tile([P, HID], BF16, tag="junk")
+                    nc.scalar.activation(out=junk[:], in_=q_raw[:, t, :], func=ACT.Square, accum_out=q_sq[:, t : t + 1])
+                q_rough = rough_reciprocal_norm(q_sq[:], Q_TILES)
+                squared_norms(0)
+
+                quantise_regrouped(0)
                 nc.vector.quantize_mx(
                     out=q_codes[:].rearrange("p c b -> p (c b)").bitcast(FP8X4),
                     scales=q_scales[:].rearrange("p c b -> p (c b)"),
                     in_=q_grouped[:].rearrange("p c b t -> p (c b t)"),
                 )
-
-            def query_norms():
-                q_sq = stats.tile([P, Q_TILES], F32)
-                for t in range(Q_TILES):
-                    junk = work.tile([P, HID], BF16, tag="junk")
-                    nc.scalar.activation(out=junk[:], in_=q_raw[:, t, :], func=ACT.Square, accum_out=q_sq[:, t : t + 1])
-                q_guess = rough_reciprocal_norm(nc, stats, q_sq[:], Q_TILES)
-                q_recip = newton_step(nc, stats, q_sq[:], q_guess, Q_TILES)
+                q_newton, q_recip, q_recip_sq = newton_steps(q_sq[:], q_rough, Q_TILES)
+                quantise_words(0)
+                regroup(1)
+                for call in q_newton[:3]:
+                    call()
                 nc.vector.tensor_scalar_mul(out=x_scale[:], in0=q_recip[:], scalar1=float(beta))
                 nc.vector.tensor_scalar_mul(out=neg_c[:], in0=q_recip[:], scalar1=-EPS)
-                c_ps = ps_st.tile([P, QUERIES], F32, tag="st")
+                quantise_regrouped(1)
+
+                gram_products(0)
+                gram_diagonals(0)
+                rough[0] = rough_reciprocal_norm(e_sq[0][:], PACK)
+                first_products(0)
+                turn_words(1)
+                c_ps = ps_yn.tile([P, QUERIES], F32, tag="yn")
                 for t in range(Q_TILES):
                     nc.tensor.matmul(
                         out=c_ps[:, t * P : (t + 1) * P],
@@ -136,258 +302,158 @@ def tile_frozenhopfield_pa_kernel(tc, q, word_embs, beta, out):
                         stop=True,
                     )
                 nc.vector.tensor_copy(out=neg_c_rows[:], in_=c_ps[:])
+                squared_norms(1)
+                newton, r, r_sq = newton_steps(e_sq[0][:], rough[0], PACK)
+                recip[0] = (r, r_sq)
+                for call in newton:
+                    call()
+                scale_rows(0)
+                load(3)
 
-            e_sq = {}
-            guess = {}
-            recip = {}
-            recip_sq = {}
-            g1 = {}
-            e1 = {}
-            st = {}
-            g_t = {}
-            y_t = {}
-            y_n = {}
-
-            def turn_words(g):
-                e_words = e_raw[g][:].bitcast(F32)
-                g1[g] = []
-                for c in range(H_PASSES):
-                    grouped = grouped_pool.tile([P, K_PASS, PACK], BF16, tag="g1", align_bytes=64)
-                    grouped_w = grouped[:].bitcast(F32)
-                    for jp in range(PACK // 2):
-                        xt = ps_xt.tile([P, 2, 2 * P], F32, tag="xt")
-                        for u in range(2):
-                            for jj in range(2):
-                                w0 = (2 * c + u) * P
-                                nc.tensor.transpose(
-                                    xt[:, u, jj * P : (jj + 1) * P], e_words[:, 2 * jp + jj, w0 : w0 + P], ident_f[:]
-                                )
-                        nc.scalar.copy(out=grouped_w[:, jp * 2 * P : (jp + 1) * 2 * P, :], in_=xt[:].rearrange("p u v -> p v u"))
-                    g1[g].append(grouped)
-
-            def squared_norms(g):
-                e_sq[g] = stats.tile([P, PACK], F32, name="e_sq")
-                for j in range(PACK):
-                    junk = work.tile([P, HID], BF16, tag="junk")
-                    nc.scalar.activation(out=junk[:], in_=e_raw[g][:, j, :], func=ACT.Square, accum_out=e_sq[g][:, j : j + 1])
-                guess[g] = rough_reciprocal_norm(nc, stats, e_sq[g][:], PACK)
-
-            def newton_steps(g):
-                factor = stats.tile([P, PACK], F32)
-                recip[g] = stats.tile([P, PACK], F32, name="recip")
-                recip_sq[g] = stats.tile([P, PACK], F32, name="recip_sq")
-                return [
-                    lambda: nc.vector.scalar_tensor_tensor(
-                        out=factor[:], in0=guess[g][:], scalar=-0.5, in1=guess[g][:], op0=ALU.mult, op1=ALU.mult
-                    ),
-                    lambda: nc.vector.tensor_mul(out=factor[:], in0=factor[:], in1=e_sq[g][:]),
-                    lambda: nc.vector.scalar_tensor_tensor(
-                        out=recip[g][:], in0=factor[:], scalar=1.5, in1=guess[g][:], op0=ALU.add, op1=ALU.mult
-                    ),
-                    lambda: nc.vector.tensor_mul(out=recip_sq[g][:], in0=recip[g][:], in1=recip[g][:]),
-                ]
-
-            def quantise_words(g, c):
-                if c == 0:
-                    codes = work.tile([P, H_PASSES, K_PASS], U32, name="e1_codes", align_bytes=64)
-                    scales = work.tile([P, H_PASSES, K_PASS], U8, name="e1_scales", align_bytes=64)
-                    e1[g] = (codes, scales)
-                codes, scales = e1[g]
-                nc.vector.quantize_mx(
-                    out=codes[:, c, :].bitcast(FP8X4),
-                    scales=scales[:, c, :],
-                    in_=g1[g][c][:].rearrange("p v t -> p (v t)"),
-                )
-
-            def first_products(g):
-                codes, scales = e1[g]
-                st[g] = []
-                for jp in range(PACK // 2):
-                    s_t = ps_st.tile([P, 2, QUERIES], F32, tag="st")
-                    for jj in range(2):
-                        j = 2 * jp + jj
-                        for c in range(H_PASSES):
-                            nc.tensor.matmul_mx(
-                                out=s_t[:, jj, :],
-                                lhsT=codes[:, c, j * P : (j + 1) * P].bitcast(FP8X4),
-                                lhsT_scale=scales[:, c, j * P : (j + 1) * P],
-                                rhs=q_codes[:, c, :].bitcast(FP8X4),
-                                rhs_scale=q_scales[:, c, :],
-                                start=(c == 0),
-                                stop=(c == H_PASSES - 1),
-                            )
-                    st[g].append(s_t)
-
-            def scale_rows(g):
-                g_t[g] = work.tile([P, PACK, QUERIES], F32, name="g_t")
-                for j in range(PACK):
-                    nc.vector.tensor_scalar(
-                        out=g_t[g][:, j, :],
-                        in0=neg_c_rows[:],
-                        scalar1=recip_sq[g][:, j : j + 1],
-                        scalar2=recip[g][:, j : j + 1],
-                        op0=ALU.mult,
-                        op1=ALU.add,
-                    )
-
-            def normalise(g, jp):
-                if jp == 0:
-                    y_t[g] = work.tile([P, PACK, QUERIES], F32, name="y_t")
-                js = slice(2 * jp, 2 * jp + 2)
-                nc.vector.tensor_tensor(out=y_t[g][:, js, :], in0=st[g][jp][:], in1=g_t[g][:, js, :], op=ALU.mult)
-
-            def turn_scores(g):
-                y_n[g] = []
-                for t in range(Q_TILES):
-                    turned = ps_yn.tile([P, BANK], F32, tag="yn")
-                    for j in range(PACK):
-                        nc.tensor.transpose(turned[:, j * P : (j + 1) * P], y_t[g][:, j, t * P : (t + 1) * P], ident_f[:])
-                    y_n[g].append(turned)
-
-            def keep_and_max(g, t):
-                nc.vector.tensor_scalar(
-                    out=x_sb[:, t, g * K_PASS : (g + 1) * K_PASS].rearrange("p (u w e) -> p u w e", u=2, e=2),
-                    in0=y_n[g][t][:].rearrange("p (u e w) -> p u w e", u=2, e=2),
-                    scalar1=x_scale[:, t : t + 1],
-                    scalar2=None,
-                    op0=ALU.mult,
-                    op1=ALU.max,
-                    accum_out=part_max[:, t, g : g + 1],
-                )
-
-            load(0)
-            nc.sync.dma_start(out=q_raw[:], in_=q.rearrange("(t p) h -> p t h", p=P))
-            load(1)
-            load(2)
-            turn_words(0)
-            quantise_queries()
-            squared_norms(0)
-            query_norms()
-            regroup_for_second_matmul(0)
-            quantise_for_second_matmul(0)
-            with tc.manual_schedule(engines={mybir.EngineType.DVE}):
-                for i in range(-1, GROUPS):
-                    now = i >= 0
-                    ahead = i + 1 < GROUPS
-                    fresh = i + 2 < GROUPS
+                for i in range(GROUPS):
+                    fresh = i + 2
                     if i + 4 < GROUPS:
                         load(i + 4)
-                    if fresh:
-                        turn_words(i + 2)
-                        squared_norms(i + 2)
-                    newton = newton_steps(i + 1) if ahead else []
-                    for step in range(2):
-                        if ahead:
-                            newton[step]()
-                        if now:
-                            normalise(i, step)
-                    if now:
-                        turn_scores(i)
-                    if ahead:
-                        for c in range(H_PASSES):
-                            newton[2 + c]()
-                            quantise_words(i + 1, c)
+                    elif i + 4 == GROUPS:
+                        load(LATE[0])
+                    if i + 1 < GROUPS:
+                        gram_products(i + 1)
+                    if fresh < GROUPS:
+                        turn_words(fresh)
+                    normalise(i)
+                    turn_scores(i)
+                    newton = []
+                    if i + 1 < GROUPS:
+                        gram_diagonals(i + 1)
+                        rough[i + 1] = rough_reciprocal_norm(e_sq[i + 1][:], PACK)
+                        quantise_words(i + 1)
                         first_products(i + 1)
-                    if i + 2 < GROUPS - LATE:
-                        regroup_for_second_matmul(i + 2)
-                    if now:
-                        for t in range(Q_TILES):
-                            keep_and_max(i, t)
-                    if i + 2 < GROUPS - LATE:
-                        quantise_for_second_matmul(i + 2)
-                    if ahead:
+                        newton, r, r_sq = newton_steps(e_sq[i + 1][:], rough[i + 1], PACK)
+                        recip[i + 1] = (r, r_sq)
+                        newton[0]()
+                    side = fresh if fresh < LAST[0] and fresh not in LATE else None
+                    if side is not None:
+                        regroup(side)
+                    if i == LAST[0]:
+                        regroup(LAST[0])
+                    if i == LAST[1]:
+                        quantise_regrouped(LAST[0])
+                    for call in newton[1:2]:
+                        call()
+                    keep_and_max(i, 0)
+                    for call in newton[2:3]:
+                        call()
+                    keep_and_max(i, 1)
+                    for call in newton[3:4]:
+                        call()
+                    if side is not None:
+                        quantise_regrouped(side)
+                    if fresh < GROUPS:
+                        squared_norms(fresh)
+                    if i + 1 < GROUPS:
                         scale_rows(i + 1)
 
-        with (
-            tc.tile_pool(name="late", bufs=1) as late,
-            tc.tile_pool(name="probs", bufs=4) as probs,
-            tc.tile_pool(name="turned", bufs=2) as turned_pool,
-            tc.psum_pool(name="ps_acc", bufs=1) as ps_acc,
-            tc.psum_pool(name="ps_pt", bufs=4) as ps_pt,
-        ):
-            p_codes = late.tile([P, GROUPS, QUERIES], U32, align_bytes=64)
-            p_scales = late.tile([P, GROUPS, QUERIES], U8, align_bytes=64)
-            neg_max = late.tile([P, Q_TILES], F32)
-            nc.vector.tensor_reduce(out=neg_max[:], in_=part_max[:], axis=AXIS.X, op=ALU.max)
-            nc.vector.tensor_scalar_mul(out=neg_max[:], in0=neg_max[:], scalar1=-1.0)
-            acc = {}
-            for t in range(Q_TILES):
-                for hh in range(H_HALVES):
-                    acc[(t, hh)] = ps_acc.tile([P, BANK], F32, name="acc%d%d" % (t, hh))
-
-            p_bf = {}
-
-            def exponentials(u):
-                cols = slice(u * PAIR * K_PASS, (u + 1) * PAIR * K_PASS)
+            with (
+                tc.tile_pool(name="late", bufs=1) as late,
+                tc.tile_pool(name="probs", bufs=4) as probs,
+                tc.tile_pool(name="turned", bufs=2) as turned_pool,
+                tc.psum_pool(name="ps_acc", bufs=1) as ps_acc,
+                tc.psum_pool(name="ps_pt", bufs=4) as ps_pt,
+            ):
+                p_codes = late.tile([P, GROUPS, QUERIES], U32, align_bytes=64)
+                p_scales = late.tile([P, GROUPS, QUERIES], U8, align_bytes=64)
+                neg_max = late.tile([P, Q_TILES], F32)
+                nc.vector.tensor_reduce(out=neg_max[:], in_=part_max[:], axis=AXIS.X, op=ALU.max)
+                nc.vector.tensor_scalar_mul(out=neg_max[:], in0=neg_max[:], scalar1=-1.0)
+                regroup(LAST[1])
+                acc = {}
                 for t in range(Q_TILES):
-                    p_bf[(u, t)] = probs.tile([P, PAIR * K_PASS], BF16, name="p_bf")
-                    nc.scalar.activation(
-                        out=p_bf[(u, t)][:],
-                        in_=x_sb[:, t, cols],
-                        func=ACT.Exp,
-                        bias=neg_max[:, t : t + 1],
-                        scale=1.0,
-                        accum_out=part_sum[:, t, u : u + 1],
-                    )
+                    for hh in range(H_HALVES):
+                        acc[(t, hh)] = ps_acc.tile([P, BANK], F32, name="acc%d%d" % (t, hh))
 
-            def turn_and_quantise(u):
-                p_grouped = turned_pool.tile([P, PAIR, QUERIES, PACK], BF16, align_bytes=64)
-                for gl in range(PAIR):
-                    p_t = ps_pt.tile([P, 2, QUERIES], F32, tag="pt")
-                    for half in range(2):
-                        for t in range(Q_TILES):
-                            w0 = (gl * 2 + half) * P
-                            p_words = p_bf[(u, t)][:].bitcast(F32)
-                            nc.tensor.transpose(p_t[:, half, t * P : (t + 1) * P], p_words[:, w0 : w0 + P], ident_f[:])
-                    copy_out = nc.vector.tensor_copy if gl == 0 else nc.scalar.copy
-                    copy_out(
-                        out=p_grouped[:, gl, :, :].rearrange("p b t -> p (b t)").bitcast(F32).rearrange("p (b k) -> p b k", k=2),
-                        in_=p_t[:].rearrange("p k b -> p b k"),
-                    )
-                nc.vector.quantize_mx(
-                    out=p_codes[:, u * PAIR : (u + 1) * PAIR, :].rearrange("p g b -> p (g b)").bitcast(FP8X4),
-                    scales=p_scales[:, u * PAIR : (u + 1) * PAIR, :].rearrange("p g b -> p (g b)"),
-                    in_=p_grouped[:].rearrange("p g b t -> p (g b t)"),
-                )
+                p_bf = {}
+                p_grouped = {}
 
-            def second_matmul(u):
-                for g in range(u * PAIR, (u + 1) * PAIR):
+                def exponentials(u):
+                    cols = slice(u * PAIR * K_PASS, (u + 1) * PAIR * K_PASS)
                     for t in range(Q_TILES):
-                        for hh in range(H_HALVES):
-                            nc.tensor.matmul_mx(
-                                out=acc[(t, hh)][:],
-                                lhsT=p_codes[:, g, t * P : (t + 1) * P].bitcast(FP8X4),
-                                lhsT_scale=p_scales[:, g, t * P : (t + 1) * P],
-                                rhs=e2_codes[:, g, hh * BANK : (hh + 1) * BANK].bitcast(FP8X4),
-                                rhs_scale=e2_scales[:, g, hh * BANK : (hh + 1) * BANK],
-                                start=(g == 0),
-                                stop=(g == GROUPS - 1),
-                            )
+                        p_bf[(u, t)] = probs.tile([P, PAIR * K_PASS], BF16, name="p_bf")
+                        nc.scalar.activation(
+                            out=p_bf[(u, t)][:],
+                            in_=x_sb[:, t, cols],
+                            func=ACT.Exp,
+                            bias=neg_max[:, t : t + 1],
+                            scale=1.0,
+                            accum_out=part_sum[:, t, u : u + 1],
+                        )
 
-            units = GROUPS // PAIR
-            for g in range(GROUPS - LATE, GROUPS - LATE + 3):
-                load(g)
-            exponentials(0)
-            for u in range(units + 1):
-                if u + 1 < units:
-                    exponentials(u + 1)
-                if u < LATE:
-                    regroup_for_second_matmul(GROUPS - LATE + u)
-                if u < units:
-                    turn_and_quantise(u)
-                if u < LATE:
-                    quantise_for_second_matmul(GROUPS - LATE + u)
-                    if u + 3 < LATE:
-                        load(GROUPS - LATE + u + 3)
-                if u >= 1:
-                    second_matmul(u - 1)
+                def turn_probs(u):
+                    p_grouped[u] = turned_pool.tile([P, PAIR, QUERIES, PACK], BF16, name="p_grouped", align_bytes=64)
+                    for gl in range(PAIR):
+                        p_t = ps_pt.tile([P, 2, QUERIES], F32, tag="pt")
+                        for half in range(2):
+                            for t in range(Q_TILES):
+                                w0 = (gl * 2 + half) * P
+                                p_words = p_bf[(u, t)][:].bitcast(F32)
+                                nc.tensor.transpose(p_t[:, half, t * P : (t + 1) * P], p_words[:, w0 : w0 + P], ident_f[:])
+                        copy_out = nc.vector.tensor_copy if gl == 0 else nc.scalar.copy
+                        copy_out(
+                            out=p_grouped[u][:].bitcast(F32)[:, gl, :, :],
+                            in_=p_t[:].rearrange("p k b -> p b k"),
+                        )
 
-            row_sum = late.tile([P, Q_TILES], F32)
-            nc.vector.tensor_reduce(out=row_sum[:], in_=part_sum[:], axis=AXIS.X, op=ALU.add)
-            inv_sum = late.tile([P, Q_TILES], F32)
-            nc.vector.reciprocal(out=inv_sum[:], in_=row_sum[:])
-            for t in range(Q_TILES):
-                result = probs.tile([P, HID], F32)
-                nc.vector.tensor_scalar_mul(out=result[:, 0:BANK], in0=acc[(t, 0)][:], scalar1=inv_sum[:, t : t + 1])
-                nc.scalar.activation(out=result[:, BANK:HID], in_=acc[(t, 1)][:], func=ACT.Copy, scale=inv_sum[:, t : t + 1])
-                nc.sync.dma_start(out=out[t * P : (t + 1) * P, :], in_=result[:])
+                def quantise_probs(u):
+                    nc.vector.quantize_mx(
+                        out=p_codes[:, u * PAIR : (u + 1) * PAIR, :].rearrange("p g b -> p (g b)").bitcast(FP8X4),
+                        scales=p_scales[:, u * PAIR : (u + 1) * PAIR, :].rearrange("p g b -> p (g b)"),
+                        in_=p_grouped[u][:].rearrange("p g b t -> p (g b t)"),
+                    )
+
+                def second_products(u):
+                    for t in range(Q_TILES):
+                        for g in range(u * PAIR, (u + 1) * PAIR):
+                            for hh in range(H_HALVES):
+                                nc.tensor.matmul_mx(
+                                    out=acc[(t, hh)][:],
+                                    lhsT=p_codes[:, g, t * P : (t + 1) * P].bitcast(FP8X4),
+                                    lhsT_scale=p_scales[:, g, t * P : (t + 1) * P],
+                                    rhs=e2_codes[:, g, hh * BANK : (hh + 1) * BANK].bitcast(FP8X4),
+                                    rhs_scale=e2_scales[:, g, hh * BANK : (hh + 1) * BANK],
+                                    start=(g == 0),
+                                    stop=(g == GROUPS - 1),
+                                )
+
+                halves = [(g, hh) for g in LATE for hh in range(H_HALVES)]
+                load(LATE[1])
+                load(LATE[2])
+                exponentials(0)
+                first = halves[0]
+                quantise_regrouped(LAST[1])
+                regroup(first[0], first[1] * BANK, (first[1] + 1) * BANK)
+                for u in range(UNITS):
+                    if u + 1 < UNITS:
+                        exponentials(u + 1)
+                    if u == 1:
+                        load(LATE[3])
+                    done = halves[u]
+                    quantise_regrouped(done[0], done[1] * BANK, (done[1] + 1) * BANK)
+                    turn_probs(u)
+                    if u + 1 < UNITS:
+                        nxt = halves[u + 1]
+                        regroup(nxt[0], nxt[1] * BANK, (nxt[1] + 1) * BANK)
+                    quantise_probs(u)
+                    if u >= 1:
+                        second_products(u - 1)
+                row_sum = late.tile([P, Q_TILES], F32)
+                nc.vector.tensor_reduce(out=row_sum[:], in_=part_sum[:], axis=AXIS.X, op=ALU.add)
+                inv_sum = late.tile([P, Q_TILES], F32)
+                nc.vector.reciprocal(out=inv_sum[:], in_=row_sum[:])
+                second_products(UNITS - 1)
+                for t in range(Q_TILES):
+                    for hh in range(H_HALVES):
+                        result = turned_pool.tile([P, BANK], F32, name="result%d" % hh)
+                        if hh == 0:
+                            nc.vector.tensor_scalar_mul(out=result[:], in0=acc[(t, hh)][:], scalar1=inv_sum[:, t : t + 1])
+                        else:
+                            nc.scalar.activation(out=result[:], in_=acc[(t, hh)][:], func=ACT.Copy, scale=inv_sum[:, t : t + 1])
+                        nc.sync.dma_start(out=out[t * P : (t + 1) * P, hh * BANK : (hh + 1) * BANK], in_=result[:])

@@ -29,18 +29,23 @@ UNITS = GROUPS // PAIR
 EPS = 1e-8
 TINY = 1e-30
 GRAM = (3,)
+BANKS = [(c, jp) for c in range(H_PASSES) for jp in range(PACK // 2)]
 ROWS_ON_SCALAR = 2
-LATE = (4, 7, 10, 13)
-LAST = (14, 15)
+EARLY = 2
+LATE_PAIRS = tuple((g, g + 1) for g in range(EARLY, GROUPS - 2, 2))
 
 
 def tile_frozenhopfield_pa_kernel(tc, q, word_embs, beta, out):
     nc = tc.nc
     with tc.tile_pool(name="keep", bufs=1) as keep, tc.tile_pool(name="stream", bufs=3) as stream, tc.tile_pool(
-        name="regroup", bufs=2
-    ) as regroup_pool, tc.tile_pool(name="stats", bufs=3) as stats:
+        name="regroup", bufs=3
+    ) as regroup_pool, tc.tile_pool(name="stats", bufs=4) as stats:
         ident_f = keep.tile([P, P], F32)
         make_identity(nc, ident_f[:])
+
+        warm = keep.tile([P, 1], F32)
+        nc.vector.memset(warm[:], 1.0)
+        nc.scalar.activation(out=warm[:], in_=warm[:], func=ACT.Abs_reciprocal_sqrt, bias=TINY)
 
         x_sb = keep.tile([P, Q_TILES, VOCAB], F32)
         e2_codes = keep.tile([P, GROUPS, HID], U32, align_bytes=64)
@@ -54,28 +59,38 @@ def tile_frozenhopfield_pa_kernel(tc, q, word_embs, beta, out):
         part_sum = keep.tile([P, Q_TILES, UNITS], F32)
 
         e_raw = {}
+        e_half = {}
         regrouped = {}
+
+        def word_rows(g):
+            return word_embs[g * K_PASS : (g + 1) * K_PASS, :].rearrange("(p j) h -> p j h", j=PACK)
 
         def load(g, pieces=1):
             e_raw[g] = stream.tile([P, PACK, HID], BF16, name="e_raw")
-            rows = word_embs[g * K_PASS : (g + 1) * K_PASS, :].rearrange("(p j) h -> p j h", j=PACK)
-            n = PACK // pieces
+            n = HID // pieces
             for k in range(pieces):
-                nc.sync.dma_start(out=e_raw[g][:, k * n : (k + 1) * n, :], in_=rows[:, k * n : (k + 1) * n, :])
+                nc.sync.dma_start(out=e_raw[g][:, :, k * n : (k + 1) * n], in_=word_rows(g)[:, :, k * n : (k + 1) * n])
 
-        def regroup(g, lo=0, hi=HID):
-            if lo == 0:
-                regrouped[g] = regroup_pool.tile([P, HID, PACK], BF16, name="e_regrouped", align_bytes=64)
+        def load_late(pair):
+            both = stream.tile([P, 2, PACK, BANK], BF16, name="e_half", tag="e_raw")
+            for k, g in enumerate(pair):
+                nc.sync.dma_start(out=both[:, k, :, :], in_=word_rows(g)[:, :, BANK:HID])
+                e_half[g] = both[:, k, :, :]
+
+        def regroup(g, hh):
+            regrouped[(g, hh)] = regroup_pool.tile([P, BANK, PACK], BF16, name="e_regrouped", align_bytes=64)
+            rows = e_half[g] if g in e_half else e_raw[g][:, :, hh * BANK : (hh + 1) * BANK]
             nc.vector.tensor_copy(
-                out=regrouped[g][:, lo:hi, :].rearrange("p (c i) t -> p c t i", i=4),
-                in_=e_raw[g][:, :, lo:hi].rearrange("p t (c i) -> p c t i", i=4),
+                out=regrouped[(g, hh)][:].rearrange("p (c i) t -> p c t i", i=4),
+                in_=rows.rearrange("p t (c i) -> p c t i", i=4),
             )
 
-        def quantise_regrouped(g, lo=0, hi=HID):
+        def quantise_regrouped(g, hh):
+            cols = slice(hh * BANK, (hh + 1) * BANK)
             nc.vector.quantize_mx(
-                out=e2_codes[:, g, lo:hi].bitcast(FP8X4),
-                scales=e2_scales[:, g, lo:hi],
-                in_=regrouped[g][:, lo:hi, :].rearrange("p h t -> p (h t)"),
+                out=e2_codes[:, g, cols].bitcast(FP8X4),
+                scales=e2_scales[:, g, cols],
+                in_=regrouped[(g, hh)][:].rearrange("p h t -> p (h t)"),
             )
 
         def rough_reciprocal_norm(sum_sq, width):
@@ -102,7 +117,8 @@ def tile_frozenhopfield_pa_kernel(tc, q, word_embs, beta, out):
         with tc.manual_schedule():
             with (
                 tc.tile_pool(name="work", bufs=2) as work,
-                tc.psum_pool(name="ps_xt", bufs=4) as ps_xt,
+                tc.psum_pool(name="ps_xt", bufs=3) as ps_xt,
+                tc.psum_pool(name="ps_gram", bufs=1) as ps_gram,
                 tc.psum_pool(name="ps_st", bufs=2) as ps_st,
                 tc.psum_pool(name="ps_yn", bufs=2) as ps_yn,
             ):
@@ -110,6 +126,7 @@ def tile_frozenhopfield_pa_kernel(tc, q, word_embs, beta, out):
                 gram = {}
                 rough = {}
                 recip = {}
+                turned_words = {}
                 g1 = {}
                 e1 = {}
                 st = {}
@@ -117,25 +134,30 @@ def tile_frozenhopfield_pa_kernel(tc, q, word_embs, beta, out):
                 y_t = {}
                 y_n = {}
 
-                def turn_words(g):
+                def turn_words(g, banks):
                     e_words = e_raw[g][:].bitcast(F32)
-                    g1[g] = work.tile([P, H_PASSES, K_PASS, PACK], BF16, name="g1", align_bytes=64)
-                    for c in range(H_PASSES):
-                        grouped_w = g1[g][:].bitcast(F32)[:, c, :, :]
-                        for jp in range(PACK // 2):
-                            xt = ps_xt.tile([P, 2, 2 * P], F32, tag="xt")
-                            for u in range(2):
-                                for jj in range(2):
-                                    w0 = (2 * c + u) * P
-                                    nc.tensor.transpose(
-                                        xt[:, u, jj * P : (jj + 1) * P], e_words[:, 2 * jp + jj, w0 : w0 + P], ident_f[:]
-                                    )
-                            nc.scalar.copy(
-                                out=grouped_w[:, jp * 2 * P : (jp + 1) * 2 * P, :], in_=xt[:].rearrange("p u v -> p v u")
-                            )
+                    for c, jp in banks:
+                        xt = ps_xt.tile([P, 2, 2 * P], F32, tag="xt")
+                        for u in range(2):
+                            for jj in range(2):
+                                w0 = (2 * c + u) * P
+                                nc.tensor.transpose(
+                                    xt[:, u, jj * P : (jj + 1) * P], e_words[:, 2 * jp + jj, w0 : w0 + P], ident_f[:]
+                                )
+                        turned_words[(g, c, jp)] = xt
+
+                def copy_words(g, banks):
+                    for c, jp in banks:
+                        if (c, jp) == BANKS[0]:
+                            g1[g] = work.tile([P, H_PASSES, K_PASS, PACK], BF16, name="g1", align_bytes=64)
+                        nc.scalar.copy(
+                            out=g1[g][:].bitcast(F32)[:, c, jp * 2 * P : (jp + 1) * 2 * P, :],
+                            in_=turned_words[(g, c, jp)][:].rearrange("p u v -> p v u"),
+                        )
+
 
                 def gram_products(g):
-                    gram[g] = ps_xt.tile([P, len(GRAM), P], F32, name="gram", tag="xt")
+                    gram[g] = ps_gram.tile([P, 2, P], F32, name="gram")
                     for k, j in enumerate(GRAM):
                         for c in range(H_PASSES):
                             for t in range(PACK):
@@ -200,9 +222,11 @@ def tile_frozenhopfield_pa_kernel(tc, q, word_embs, beta, out):
                                 )
                         st[g].append(s_t)
 
-                def scale_rows(g):
-                    r, r_sq = recip[g]
+                def start_factors(g):
                     g_t[g] = work.tile([P, PACK, QUERIES], F32, name="g_t", align_bytes=64)
+
+                def factors_on_scalar(g):
+                    r, r_sq = recip[g]
                     for j in range(ROWS_ON_SCALAR):
                         nc.scalar.activation(
                             out=g_t[g][:, j, :],
@@ -211,6 +235,9 @@ def tile_frozenhopfield_pa_kernel(tc, q, word_embs, beta, out):
                             scale=r_sq[:, j : j + 1],
                             bias=r[:, j : j + 1],
                         )
+
+                def factors_on_vector(g):
+                    r, r_sq = recip[g]
                     for j in range(ROWS_ON_SCALAR, PACK):
                         nc.vector.tensor_scalar(
                             out=g_t[g][:, j, :],
@@ -221,11 +248,11 @@ def tile_frozenhopfield_pa_kernel(tc, q, word_embs, beta, out):
                             op1=ALU.add,
                         )
 
-                def normalise(g):
-                    y_t[g] = work.tile([P, PACK, QUERIES], F32, name="y_t")
-                    for jp in range(PACK // 2):
-                        js = slice(2 * jp, 2 * jp + 2)
-                        nc.vector.tensor_tensor(out=y_t[g][:, js, :], in0=st[g][jp][:], in1=g_t[g][:, js, :], op=ALU.mult)
+                def normalise(g, jp):
+                    if jp == 0:
+                        y_t[g] = work.tile([P, PACK, QUERIES], F32, name="y_t")
+                    js = slice(2 * jp, 2 * jp + 2)
+                    nc.vector.tensor_tensor(out=y_t[g][:, js, :], in0=st[g][jp][:], in1=g_t[g][:, js, :], op=ALU.mult)
 
                 def turn_scores(g):
                     y_n[g] = []
@@ -235,25 +262,30 @@ def tile_frozenhopfield_pa_kernel(tc, q, word_embs, beta, out):
                             nc.tensor.transpose(turned[:, j * P : (j + 1) * P], y_t[g][:, j, t * P : (t + 1) * P], ident_f[:])
                         y_n[g].append(turned)
 
-                def keep_and_max(g, t):
-                    nc.vector.tensor_scalar(
-                        out=x_sb[:, t, g * K_PASS : (g + 1) * K_PASS].rearrange("p (u w e) -> p u w e", u=2, e=2),
-                        in0=y_n[g][t][:].rearrange("p (u e w) -> p u w e", u=2, e=2),
-                        scalar1=x_scale[:, t : t + 1],
-                        scalar2=None,
-                        op0=ALU.mult,
-                        op1=ALU.max,
-                        accum_out=part_max[:, t, g : g + 1],
-                    )
+                def keep_and_max(g):
+                    for t in range(Q_TILES):
+                        nc.vector.tensor_scalar(
+                            out=x_sb[:, t, g * K_PASS : (g + 1) * K_PASS].rearrange("p (u w e) -> p u w e", u=2, e=2),
+                            in0=y_n[g][t][:].rearrange("p (u e w) -> p u w e", u=2, e=2),
+                            scalar1=x_scale[:, t : t + 1],
+                            scalar2=None,
+                            op0=ALU.mult,
+                            op1=ALU.max,
+                            accum_out=part_max[:, t, g : g + 1],
+                        )
 
-                load(0, pieces=PACK)
+                load(0, pieces=H_HALVES)
                 q_raw = work.tile([P, Q_TILES, HID], BF16, tag="y_t")
                 nc.sync.dma_start(out=q_raw[:], in_=q.rearrange("(t p) h -> p t h", p=P))
                 load(1)
                 load(2)
 
-                turn_words(0)
-                regroup(0)
+                turn_words(0, BANKS[:3])
+                copy_words(0, BANKS[:1])
+                turn_words(0, BANKS[3:])
+                copy_words(0, BANKS[1:])
+                regroup(0, 0)
+                regroup(0, 1)
 
                 q_words = q_raw[:].bitcast(F32)
                 q_grouped = work.tile([P, H_PASSES, QUERIES, PACK], BF16, tag="g_t", align_bytes=64)
@@ -264,6 +296,7 @@ def tile_frozenhopfield_pa_kernel(tc, q, word_embs, beta, out):
                             w0 = (2 * c + u) * P
                             nc.tensor.transpose(xt[:, u, t * P : (t + 1) * P], q_words[:, t, w0 : w0 + P], ident_f[:])
                     nc.scalar.copy(out=q_grouped[:].bitcast(F32)[:, c, :, :], in_=xt[:].rearrange("p u b -> p b u"))
+                gram_products(0)
 
                 q_sq = stats.tile([P, Q_TILES], F32)
                 for t in range(Q_TILES):
@@ -272,26 +305,31 @@ def tile_frozenhopfield_pa_kernel(tc, q, word_embs, beta, out):
                 q_rough = rough_reciprocal_norm(q_sq[:], Q_TILES)
                 squared_norms(0)
 
-                quantise_regrouped(0)
+                quantise_regrouped(0, 0)
+                quantise_words(0)
+                quantise_regrouped(0, 1)
                 nc.vector.quantize_mx(
                     out=q_codes[:].rearrange("p c b -> p (c b)").bitcast(FP8X4),
                     scales=q_scales[:].rearrange("p c b -> p (c b)"),
                     in_=q_grouped[:].rearrange("p c b t -> p (c b t)"),
                 )
-                q_newton, q_recip, q_recip_sq = newton_steps(q_sq[:], q_rough, Q_TILES)
-                quantise_words(0)
-                regroup(1)
-                for call in q_newton[:3]:
-                    call()
-                nc.vector.tensor_scalar_mul(out=x_scale[:], in0=q_recip[:], scalar1=float(beta))
-                nc.vector.tensor_scalar_mul(out=neg_c[:], in0=q_recip[:], scalar1=-EPS)
-                quantise_regrouped(1)
-
-                gram_products(0)
-                gram_diagonals(0)
-                rough[0] = rough_reciprocal_norm(e_sq[0][:], PACK)
                 first_products(0)
-                turn_words(1)
+                gram_diagonals(0)
+                q_newton, q_recip, q_recip_sq = newton_steps(q_sq[:], q_rough, Q_TILES)
+                for call in q_newton[:1]:
+                    call()
+                regroup(1, 0)
+                for call in q_newton[1:2]:
+                    call()
+                regroup(1, 1)
+                for call in q_newton[2:3]:
+                    call()
+                quantise_regrouped(1, 0)
+                nc.vector.tensor_scalar_mul(out=neg_c[:], in0=q_recip[:], scalar1=-EPS)
+                nc.vector.tensor_scalar_mul(out=x_scale[:], in0=q_recip[:], scalar1=float(beta))
+                quantise_regrouped(1, 1)
+
+                turn_words(1, BANKS[:3])
                 c_ps = ps_yn.tile([P, QUERIES], F32, tag="yn")
                 for t in range(Q_TILES):
                     nc.tensor.matmul(
@@ -302,56 +340,67 @@ def tile_frozenhopfield_pa_kernel(tc, q, word_embs, beta, out):
                         stop=True,
                     )
                 nc.vector.tensor_copy(out=neg_c_rows[:], in_=c_ps[:])
-                squared_norms(1)
-                newton, r, r_sq = newton_steps(e_sq[0][:], rough[0], PACK)
-                recip[0] = (r, r_sq)
-                for call in newton:
-                    call()
-                scale_rows(0)
                 load(3)
 
-                for i in range(GROUPS):
-                    fresh = i + 2
-                    if i + 4 < GROUPS:
-                        load(i + 4)
-                    elif i + 4 == GROUPS:
-                        load(LATE[0])
-                    if i + 1 < GROUPS:
-                        gram_products(i + 1)
-                    if fresh < GROUPS:
-                        turn_words(fresh)
-                    normalise(i)
-                    turn_scores(i)
-                    newton = []
-                    if i + 1 < GROUPS:
-                        gram_diagonals(i + 1)
+                for i in range(-1, GROUPS):
+                    now = i >= 0
+                    ahead = i + 1 < GROUPS
+                    fresh = i + 2 < GROUPS
+                    side = (i + 2, 0) if fresh else (i, 1)
+                    if now:
+                        if i + 4 < GROUPS:
+                            load(i + 4)
+                        elif i + 4 == GROUPS:
+                            load_late(LATE_PAIRS[0])
+
+                    if fresh:
+                        turn_words(i + 2, BANKS[3:])
+                        copy_words(i + 2, BANKS[:1])
+                    if ahead:
                         rough[i + 1] = rough_reciprocal_norm(e_sq[i + 1][:], PACK)
-                        quantise_words(i + 1)
-                        first_products(i + 1)
                         newton, r, r_sq = newton_steps(e_sq[i + 1][:], rough[i + 1], PACK)
                         recip[i + 1] = (r, r_sq)
-                        newton[0]()
-                    side = fresh if fresh < LAST[0] and fresh not in LATE else None
-                    if side is not None:
-                        regroup(side)
-                    if i == LAST[0]:
-                        regroup(LAST[0])
-                    if i == LAST[1]:
-                        quantise_regrouped(LAST[0])
+                    else:
+                        newton = []
+                    if fresh:
+                        copy_words(i + 2, BANKS[1:])
+                        gram_products(i + 2)
+                    if i + 3 < GROUPS:
+                        turn_words(i + 3, BANKS[:3])
+                    if ahead and now:
+                        quantise_words(i + 1)
+                    if now:
+                        start_factors(i)
+                        factors_on_scalar(i)
+                        factors_on_vector(i)
+                    if i == GROUPS - 1:
+                        nc.scalar.activation(out=warm[:], in_=warm[:], func=ACT.Exp)
+                    if fresh:
+                        squared_norms(i + 2)
+                    if i > 0:
+                        keep_and_max(i - 1)
+                    for call in newton[0:1]:
+                        call()
+                    if now:
+                        regroup(*side)
                     for call in newton[1:2]:
                         call()
-                    keep_and_max(i, 0)
+                    if now:
+                        normalise(i, 0)
                     for call in newton[2:3]:
                         call()
-                    keep_and_max(i, 1)
+                    if now:
+                        normalise(i, 1)
+                        turn_scores(i)
                     for call in newton[3:4]:
                         call()
-                    if side is not None:
-                        quantise_regrouped(side)
-                    if fresh < GROUPS:
-                        squared_norms(fresh)
-                    if i + 1 < GROUPS:
-                        scale_rows(i + 1)
+                    if ahead and now:
+                        first_products(i + 1)
+                    if fresh:
+                        gram_diagonals(i + 2)
+                    if now and i < GROUPS - 1:
+                        quantise_regrouped(*side)
+                keep_and_max(GROUPS - 1)
 
             with (
                 tc.tile_pool(name="late", bufs=1) as late,
@@ -365,7 +414,7 @@ def tile_frozenhopfield_pa_kernel(tc, q, word_embs, beta, out):
                 neg_max = late.tile([P, Q_TILES], F32)
                 nc.vector.tensor_reduce(out=neg_max[:], in_=part_max[:], axis=AXIS.X, op=ALU.max)
                 nc.vector.tensor_scalar_mul(out=neg_max[:], in0=neg_max[:], scalar1=-1.0)
-                regroup(LAST[1])
+                quantise_regrouped(GROUPS - 1, 1)
                 acc = {}
                 for t in range(Q_TILES):
                     for hh in range(H_HALVES):
@@ -396,8 +445,7 @@ def tile_frozenhopfield_pa_kernel(tc, q, word_embs, beta, out):
                                 w0 = (gl * 2 + half) * P
                                 p_words = p_bf[(u, t)][:].bitcast(F32)
                                 nc.tensor.transpose(p_t[:, half, t * P : (t + 1) * P], p_words[:, w0 : w0 + P], ident_f[:])
-                        copy_out = nc.vector.tensor_copy if gl == 0 else nc.scalar.copy
-                        copy_out(
+                        nc.scalar.copy(
                             out=p_grouped[u][:].bitcast(F32)[:, gl, :, :],
                             in_=p_t[:].rearrange("p k b -> p b k"),
                         )
@@ -423,25 +471,28 @@ def tile_frozenhopfield_pa_kernel(tc, q, word_embs, beta, out):
                                     stop=(g == GROUPS - 1),
                                 )
 
-                halves = [(g, hh) for g in LATE for hh in range(H_HALVES)]
-                load(LATE[1])
-                load(LATE[2])
+                load_late(LATE_PAIRS[1])
+                load_late(LATE_PAIRS[2])
                 exponentials(0)
-                first = halves[0]
-                quantise_regrouped(LAST[1])
-                regroup(first[0], first[1] * BANK, (first[1] + 1) * BANK)
-                for u in range(UNITS):
-                    if u + 1 < UNITS:
+                halves = [g for pair in LATE_PAIRS for g in pair]
+                loads = 3
+                done = 0
+                for u in range(-1, UNITS):
+                    share = 2 if u in (-1, 0, 1, 4) else 1
+                    batch = halves[done : done + share]
+                    done += share
+                    if u + 1 < UNITS and u >= 0:
                         exponentials(u + 1)
-                    if u == 1:
-                        load(LATE[3])
-                    done = halves[u]
-                    quantise_regrouped(done[0], done[1] * BANK, (done[1] + 1) * BANK)
-                    turn_probs(u)
-                    if u + 1 < UNITS:
-                        nxt = halves[u + 1]
-                        regroup(nxt[0], nxt[1] * BANK, (nxt[1] + 1) * BANK)
-                    quantise_probs(u)
+                    for g in batch:
+                        regroup(g, 1)
+                    if u >= 0:
+                        turn_probs(u)
+                        quantise_probs(u)
+                    for g in batch:
+                        quantise_regrouped(g, 1)
+                    if loads < len(LATE_PAIRS) and done >= 2 * (loads - 2):
+                        load_late(LATE_PAIRS[loads])
+                        loads += 1
                     if u >= 1:
                         second_products(u - 1)
                 row_sum = late.tile([P, Q_TILES], F32)

@@ -25,12 +25,12 @@ H_PASSES = HID // K_PASS
 GROUPS = VOCAB // K_PASS
 H_HALVES = HID // BANK
 PAIR = 2
-UNITS = GROUPS // PAIR
+UNITS = [(g, g + 1) for g in range(0, GROUPS - PAIR, PAIR)] + [(GROUPS - 2,), (GROUPS - 1,)]
 EPS = 1e-8
 TINY = 1e-30
 GRAM = (3,)
 BANKS = [(c, jp) for c in range(H_PASSES) for jp in range(PACK // 2)]
-ROWS_ON_SCALAR = 2
+ROWS_ON_SCALAR = 1
 EARLY = 2
 LATE_PAIRS = tuple((g, g + 1) for g in range(EARLY, GROUPS - 2, 2))
 
@@ -38,7 +38,7 @@ LATE_PAIRS = tuple((g, g + 1) for g in range(EARLY, GROUPS - 2, 2))
 def tile_frozenhopfield_pa_kernel(tc, q, word_embs, beta, out):
     nc = tc.nc
     with tc.tile_pool(name="keep", bufs=1) as keep, tc.tile_pool(name="stream", bufs=3) as stream, tc.tile_pool(
-        name="regroup", bufs=3
+        name="regroup", bufs=4
     ) as regroup_pool, tc.tile_pool(name="stats", bufs=4) as stats:
         ident_f = keep.tile([P, P], F32)
         make_identity(nc, ident_f[:])
@@ -56,7 +56,7 @@ def tile_frozenhopfield_pa_kernel(tc, q, word_embs, beta, out):
         x_scale = keep.tile([P, Q_TILES], F32)
         neg_c = keep.tile([P, Q_TILES], F32)
         part_max = keep.tile([P, Q_TILES, GROUPS], F32)
-        part_sum = keep.tile([P, Q_TILES, UNITS], F32)
+        part_sum = keep.tile([P, Q_TILES, len(UNITS)], F32, name="part_sum")
 
         e_raw = {}
         e_half = {}
@@ -77,10 +77,10 @@ def tile_frozenhopfield_pa_kernel(tc, q, word_embs, beta, out):
                 nc.sync.dma_start(out=both[:, k, :, :], in_=word_rows(g)[:, :, BANK:HID])
                 e_half[g] = both[:, k, :, :]
 
-        def regroup(g, hh):
+        def regroup(g, hh, copy=nc.vector.tensor_copy):
             regrouped[(g, hh)] = regroup_pool.tile([P, BANK, PACK], BF16, name="e_regrouped", align_bytes=64)
             rows = e_half[g] if g in e_half else e_raw[g][:, :, hh * BANK : (hh + 1) * BANK]
-            nc.vector.tensor_copy(
+            copy(
                 out=regrouped[(g, hh)][:].rearrange("p (c i) t -> p c t i", i=4),
                 in_=rows.rearrange("p t (c i) -> p c t i", i=4),
             )
@@ -296,12 +296,21 @@ def tile_frozenhopfield_pa_kernel(tc, q, word_embs, beta, out):
                             w0 = (2 * c + u) * P
                             nc.tensor.transpose(xt[:, u, t * P : (t + 1) * P], q_words[:, t, w0 : w0 + P], ident_f[:])
                     nc.scalar.copy(out=q_grouped[:].bitcast(F32)[:, c, :, :], in_=xt[:].rearrange("p u b -> p b u"))
+                turn_words(1, BANKS[:3])
                 gram_products(0)
 
                 q_sq = stats.tile([P, Q_TILES], F32)
                 for t in range(Q_TILES):
                     junk = work.tile([P, HID], BF16, tag="junk")
-                    nc.scalar.activation(out=junk[:], in_=q_raw[:, t, :], func=ACT.Square, accum_out=q_sq[:, t : t + 1])
+                    nc.vector.scalar_tensor_tensor(
+                        out=junk[:],
+                        in0=q_raw[:, t, :],
+                        scalar=1.0,
+                        in1=q_raw[:, t, :],
+                        op0=ALU.mult,
+                        op1=ALU.mult,
+                        accum_out=q_sq[:, t : t + 1],
+                    )
                 q_rough = rough_reciprocal_norm(q_sq[:], Q_TILES)
                 squared_norms(0)
 
@@ -329,17 +338,19 @@ def tile_frozenhopfield_pa_kernel(tc, q, word_embs, beta, out):
                 nc.vector.tensor_scalar_mul(out=x_scale[:], in0=q_recip[:], scalar1=float(beta))
                 quantise_regrouped(1, 1)
 
-                turn_words(1, BANKS[:3])
-                c_ps = ps_yn.tile([P, QUERIES], F32, tag="yn")
-                for t in range(Q_TILES):
-                    nc.tensor.matmul(
-                        out=c_ps[:, t * P : (t + 1) * P],
-                        lhsT=neg_c[:, t : t + 1].to_broadcast([P, P]),
-                        rhs=ident_f[:],
-                        start=True,
-                        stop=True,
-                    )
-                nc.vector.tensor_copy(out=neg_c_rows[:], in_=c_ps[:])
+
+                def spread_query_norms():
+                    c_ps = ps_yn.tile([P, QUERIES], F32, tag="yn")
+                    for t in range(Q_TILES):
+                        nc.tensor.matmul(
+                            out=c_ps[:, t * P : (t + 1) * P],
+                            lhsT=neg_c[:, t : t + 1].to_broadcast([P, P]),
+                            rhs=ident_f[:],
+                            start=True,
+                            stop=True,
+                        )
+                    nc.vector.tensor_copy(out=neg_c_rows[:], in_=c_ps[:])
+
                 load(3)
 
                 for i in range(-1, GROUPS):
@@ -373,15 +384,20 @@ def tile_frozenhopfield_pa_kernel(tc, q, word_embs, beta, out):
                         start_factors(i)
                         factors_on_scalar(i)
                         factors_on_vector(i)
+                    if i == GROUPS - 2:
+                        for g in (GROUPS - 2, GROUPS - 1):
+                            regroup(g, 1, nc.scalar.copy)
                     if i == GROUPS - 1:
                         nc.scalar.activation(out=warm[:], in_=warm[:], func=ACT.Exp)
+                        for g in LATE_PAIRS[0]:
+                            regroup(g, 1, nc.scalar.copy)
                     if fresh:
                         squared_norms(i + 2)
                     if i > 0:
                         keep_and_max(i - 1)
                     for call in newton[0:1]:
                         call()
-                    if now:
+                    if now and fresh:
                         regroup(*side)
                     for call in newton[1:2]:
                         call()
@@ -398,7 +414,9 @@ def tile_frozenhopfield_pa_kernel(tc, q, word_embs, beta, out):
                         first_products(i + 1)
                     if fresh:
                         gram_diagonals(i + 2)
-                    if now and i < GROUPS - 1:
+                    if not now:
+                        spread_query_norms()
+                    if now and fresh:
                         quantise_regrouped(*side)
                 keep_and_max(GROUPS - 1)
 
@@ -414,7 +432,8 @@ def tile_frozenhopfield_pa_kernel(tc, q, word_embs, beta, out):
                 neg_max = late.tile([P, Q_TILES], F32)
                 nc.vector.tensor_reduce(out=neg_max[:], in_=part_max[:], axis=AXIS.X, op=ALU.max)
                 nc.vector.tensor_scalar_mul(out=neg_max[:], in0=neg_max[:], scalar1=-1.0)
-                quantise_regrouped(GROUPS - 1, 1)
+                for g in (GROUPS - 2, GROUPS - 1):
+                    quantise_regrouped(g, 1)
                 acc = {}
                 for t in range(Q_TILES):
                     for hh in range(H_HALVES):
@@ -424,11 +443,12 @@ def tile_frozenhopfield_pa_kernel(tc, q, word_embs, beta, out):
                 p_grouped = {}
 
                 def exponentials(u):
-                    cols = slice(u * PAIR * K_PASS, (u + 1) * PAIR * K_PASS)
+                    cols = slice(UNITS[u][0] * K_PASS, (UNITS[u][-1] + 1) * K_PASS)
+                    width = len(UNITS[u]) * K_PASS
                     for t in range(Q_TILES):
                         p_bf[(u, t)] = probs.tile([P, PAIR * K_PASS], BF16, name="p_bf")
                         nc.scalar.activation(
-                            out=p_bf[(u, t)][:],
+                            out=p_bf[(u, t)][:, 0:width],
                             in_=x_sb[:, t, cols],
                             func=ACT.Exp,
                             bias=neg_max[:, t : t + 1],
@@ -438,7 +458,7 @@ def tile_frozenhopfield_pa_kernel(tc, q, word_embs, beta, out):
 
                 def turn_probs(u):
                     p_grouped[u] = turned_pool.tile([P, PAIR, QUERIES, PACK], BF16, name="p_grouped", align_bytes=64)
-                    for gl in range(PAIR):
+                    for gl in range(len(UNITS[u])):
                         p_t = ps_pt.tile([P, 2, QUERIES], F32, tag="pt")
                         for half in range(2):
                             for t in range(Q_TILES):
@@ -451,15 +471,16 @@ def tile_frozenhopfield_pa_kernel(tc, q, word_embs, beta, out):
                         )
 
                 def quantise_probs(u):
+                    gs = slice(UNITS[u][0], UNITS[u][-1] + 1)
                     nc.vector.quantize_mx(
-                        out=p_codes[:, u * PAIR : (u + 1) * PAIR, :].rearrange("p g b -> p (g b)").bitcast(FP8X4),
-                        scales=p_scales[:, u * PAIR : (u + 1) * PAIR, :].rearrange("p g b -> p (g b)"),
-                        in_=p_grouped[u][:].rearrange("p g b t -> p (g b t)"),
+                        out=p_codes[:, gs, :].rearrange("p g b -> p (g b)").bitcast(FP8X4),
+                        scales=p_scales[:, gs, :].rearrange("p g b -> p (g b)"),
+                        in_=p_grouped[u][:, 0 : len(UNITS[u]), :, :].rearrange("p g b t -> p (g b t)"),
                     )
 
                 def second_products(u):
                     for t in range(Q_TILES):
-                        for g in range(u * PAIR, (u + 1) * PAIR):
+                        for g in UNITS[u]:
                             for hh in range(H_HALVES):
                                 nc.tensor.matmul_mx(
                                     out=acc[(t, hh)][:],
@@ -477,14 +498,15 @@ def tile_frozenhopfield_pa_kernel(tc, q, word_embs, beta, out):
                 halves = [g for pair in LATE_PAIRS for g in pair]
                 loads = 3
                 done = 0
-                for u in range(-1, UNITS):
+                for u in range(-1, len(UNITS)):
                     share = 2 if u in (-1, 0, 1, 4) else 1
                     batch = halves[done : done + share]
                     done += share
-                    if u + 1 < UNITS and u >= 0:
+                    if u + 1 < len(UNITS) and u >= 0:
                         exponentials(u + 1)
                     for g in batch:
-                        regroup(g, 1)
+                        if u >= 0:
+                            regroup(g, 1)
                     if u >= 0:
                         turn_probs(u)
                         quantise_probs(u)
@@ -499,7 +521,7 @@ def tile_frozenhopfield_pa_kernel(tc, q, word_embs, beta, out):
                 nc.vector.tensor_reduce(out=row_sum[:], in_=part_sum[:], axis=AXIS.X, op=ALU.add)
                 inv_sum = late.tile([P, Q_TILES], F32)
                 nc.vector.reciprocal(out=inv_sum[:], in_=row_sum[:])
-                second_products(UNITS - 1)
+                second_products(len(UNITS) - 1)
                 for t in range(Q_TILES):
                     for hh in range(H_HALVES):
                         result = turned_pool.tile([P, BANK], F32, name="result%d" % hh)

@@ -31,6 +31,7 @@ TINY = 1e-30
 GRAM = (3,)
 BANKS = [(c, jp) for c in range(H_PASSES) for jp in range(PACK // 2)]
 ROWS_ON_SCALAR = 1
+ROWS_ON_VECTOR = 1
 EARLY = 2
 LATE_PAIRS = tuple((g, g + 1) for g in range(EARLY, GROUPS - 2, 2))
 
@@ -124,6 +125,7 @@ def tile_frozenhopfield_pa_kernel(tc, q, word_embs, beta, out):
             ):
                 e_sq = {}
                 gram = {}
+                last_newton = {}
                 rough = {}
                 recip = {}
                 turned_words = {}
@@ -238,8 +240,20 @@ def tile_frozenhopfield_pa_kernel(tc, q, word_embs, beta, out):
 
                 def factors_on_vector(g):
                     r, r_sq = recip[g]
-                    for j in range(ROWS_ON_SCALAR, PACK):
+                    for j in range(PACK - ROWS_ON_VECTOR, PACK):
                         nc.vector.tensor_scalar(
+                            out=g_t[g][:, j, :],
+                            in0=neg_c_rows[:],
+                            scalar1=r_sq[:, j : j + 1],
+                            scalar2=r[:, j : j + 1],
+                            op0=ALU.mult,
+                            op1=ALU.add,
+                        )
+
+                def factors_on_gpsimd(g):
+                    r, r_sq = recip[g]
+                    for j in range(ROWS_ON_SCALAR, PACK - ROWS_ON_VECTOR):
+                        nc.gpsimd.tensor_scalar(
                             out=g_t[g][:, j, :],
                             in0=neg_c_rows[:],
                             scalar1=r_sq[:, j : j + 1],
@@ -371,6 +385,7 @@ def tile_frozenhopfield_pa_kernel(tc, q, word_embs, beta, out):
                         rough[i + 1] = rough_reciprocal_norm(e_sq[i + 1][:], PACK)
                         newton, r, r_sq = newton_steps(e_sq[i + 1][:], rough[i + 1], PACK)
                         recip[i + 1] = (r, r_sq)
+                        last_newton[i + 1] = newton[3]
                     else:
                         newton = []
                     if fresh:
@@ -382,8 +397,9 @@ def tile_frozenhopfield_pa_kernel(tc, q, word_embs, beta, out):
                         quantise_words(i + 1)
                     if now:
                         start_factors(i)
+                        last_newton[i]()
                         factors_on_scalar(i)
-                        factors_on_vector(i)
+                        factors_on_gpsimd(i)
                     if i == GROUPS - 2:
                         for g in (GROUPS - 2, GROUPS - 1):
                             regroup(g, 1, nc.scalar.copy)
@@ -395,6 +411,8 @@ def tile_frozenhopfield_pa_kernel(tc, q, word_embs, beta, out):
                         squared_norms(i + 2)
                     if i > 0:
                         keep_and_max(i - 1)
+                    if now:
+                        factors_on_vector(i)
                     for call in newton[0:1]:
                         call()
                     if now and fresh:
@@ -408,8 +426,6 @@ def tile_frozenhopfield_pa_kernel(tc, q, word_embs, beta, out):
                     if now:
                         normalise(i, 1)
                         turn_scores(i)
-                    for call in newton[3:4]:
-                        call()
                     if ahead and now:
                         first_products(i + 1)
                     if fresh:
@@ -465,7 +481,8 @@ def tile_frozenhopfield_pa_kernel(tc, q, word_embs, beta, out):
                                 w0 = (gl * 2 + half) * P
                                 p_words = p_bf[(u, t)][:].bitcast(F32)
                                 nc.tensor.transpose(p_t[:, half, t * P : (t + 1) * P], p_words[:, w0 : w0 + P], ident_f[:])
-                        nc.scalar.copy(
+                        copy_out = nc.vector.tensor_copy if u == 0 else nc.scalar.copy
+                        copy_out(
                             out=p_grouped[u][:].bitcast(F32)[:, gl, :, :],
                             in_=p_t[:].rearrange("p k b -> p b k"),
                         )
@@ -515,12 +532,13 @@ def tile_frozenhopfield_pa_kernel(tc, q, word_embs, beta, out):
                     if loads < len(LATE_PAIRS) and done >= 2 * (loads - 2):
                         load_late(LATE_PAIRS[loads])
                         loads += 1
-                    if u >= 1:
-                        second_products(u - 1)
+                    if u >= 2:
+                        second_products(u - 2)
                 row_sum = late.tile([P, Q_TILES], F32)
                 nc.vector.tensor_reduce(out=row_sum[:], in_=part_sum[:], axis=AXIS.X, op=ALU.add)
                 inv_sum = late.tile([P, Q_TILES], F32)
                 nc.vector.reciprocal(out=inv_sum[:], in_=row_sum[:])
+                second_products(len(UNITS) - 2)
                 second_products(len(UNITS) - 1)
                 for t in range(Q_TILES):
                     for hh in range(H_HALVES):

@@ -30,8 +30,8 @@ EPS = 1e-8
 TINY = 1e-30
 GRAM = (3,)
 BANKS = [(c, jp) for c in range(H_PASSES) for jp in range(PACK // 2)]
-ROWS_ON_SCALAR = 1
-ROWS_ON_VECTOR = 1
+ROWS_ON_SCALAR = (1, 0)
+ROWS_ON_VECTOR = (0, 1)
 EARLY = 2
 LATE_PAIRS = tuple((g, g + 1) for g in range(EARLY, GROUPS - 2, 2))
 
@@ -56,7 +56,7 @@ def tile_frozenhopfield_pa_kernel(tc, q, word_embs, beta, out):
         neg_c_rows = keep.tile([P, QUERIES], F32)
         x_scale = keep.tile([P, Q_TILES], F32)
         neg_c = keep.tile([P, Q_TILES], F32)
-        part_max = keep.tile([P, Q_TILES, GROUPS], F32)
+        part_min = keep.tile([P, Q_TILES, GROUPS], F32)
         part_sum = keep.tile([P, Q_TILES, len(UNITS)], F32, name="part_sum")
 
         e_raw = {}
@@ -229,7 +229,7 @@ def tile_frozenhopfield_pa_kernel(tc, q, word_embs, beta, out):
 
                 def factors_on_scalar(g):
                     r, r_sq = recip[g]
-                    for j in range(ROWS_ON_SCALAR):
+                    for j in range(ROWS_ON_SCALAR[g % 2]):
                         nc.scalar.activation(
                             out=g_t[g][:, j, :],
                             in_=neg_c_rows[:],
@@ -240,7 +240,7 @@ def tile_frozenhopfield_pa_kernel(tc, q, word_embs, beta, out):
 
                 def factors_on_vector(g):
                     r, r_sq = recip[g]
-                    for j in range(PACK - ROWS_ON_VECTOR, PACK):
+                    for j in range(PACK - ROWS_ON_VECTOR[g % 2], PACK):
                         nc.vector.tensor_scalar(
                             out=g_t[g][:, j, :],
                             in0=neg_c_rows[:],
@@ -252,7 +252,7 @@ def tile_frozenhopfield_pa_kernel(tc, q, word_embs, beta, out):
 
                 def factors_on_gpsimd(g):
                     r, r_sq = recip[g]
-                    for j in range(ROWS_ON_SCALAR, PACK - ROWS_ON_VECTOR):
+                    for j in range(ROWS_ON_SCALAR[g % 2], PACK - ROWS_ON_VECTOR[g % 2]):
                         nc.gpsimd.tensor_scalar(
                             out=g_t[g][:, j, :],
                             in0=neg_c_rows[:],
@@ -276,7 +276,7 @@ def tile_frozenhopfield_pa_kernel(tc, q, word_embs, beta, out):
                             nc.tensor.transpose(turned[:, j * P : (j + 1) * P], y_t[g][:, j, t * P : (t + 1) * P], ident_f[:])
                         y_n[g].append(turned)
 
-                def keep_and_max(g):
+                def keep_and_min(g):
                     for t in range(Q_TILES):
                         nc.vector.tensor_scalar(
                             out=x_sb[:, t, g * K_PASS : (g + 1) * K_PASS].rearrange("p (u w e) -> p u w e", u=2, e=2),
@@ -284,8 +284,8 @@ def tile_frozenhopfield_pa_kernel(tc, q, word_embs, beta, out):
                             scalar1=x_scale[:, t : t + 1],
                             scalar2=None,
                             op0=ALU.mult,
-                            op1=ALU.max,
-                            accum_out=part_max[:, t, g : g + 1],
+                            op1=ALU.min,
+                            accum_out=part_min[:, t, g : g + 1],
                         )
 
                 load(0, pieces=H_HALVES)
@@ -349,7 +349,7 @@ def tile_frozenhopfield_pa_kernel(tc, q, word_embs, beta, out):
                     call()
                 quantise_regrouped(1, 0)
                 nc.vector.tensor_scalar_mul(out=neg_c[:], in0=q_recip[:], scalar1=-EPS)
-                nc.vector.tensor_scalar_mul(out=x_scale[:], in0=q_recip[:], scalar1=float(beta))
+                nc.vector.tensor_scalar_mul(out=x_scale[:], in0=q_recip[:], scalar1=-float(beta))
                 quantise_regrouped(1, 1)
 
 
@@ -393,11 +393,12 @@ def tile_frozenhopfield_pa_kernel(tc, q, word_embs, beta, out):
                         gram_products(i + 2)
                     if i + 3 < GROUPS:
                         turn_words(i + 3, BANKS[:3])
+                    if now:
+                        last_newton[i]()
                     if ahead and now:
                         quantise_words(i + 1)
                     if now:
                         start_factors(i)
-                        last_newton[i]()
                         factors_on_scalar(i)
                         factors_on_gpsimd(i)
                     if i == GROUPS - 2:
@@ -405,12 +406,11 @@ def tile_frozenhopfield_pa_kernel(tc, q, word_embs, beta, out):
                             regroup(g, 1, nc.scalar.copy)
                     if i == GROUPS - 1:
                         nc.scalar.activation(out=warm[:], in_=warm[:], func=ACT.Exp)
-                        for g in LATE_PAIRS[0]:
-                            regroup(g, 1, nc.scalar.copy)
+                        regroup(LATE_PAIRS[0][0], 1, nc.scalar.copy)
                     if fresh:
                         squared_norms(i + 2)
                     if i > 0:
-                        keep_and_max(i - 1)
+                        keep_and_min(i - 1)
                     if now:
                         factors_on_vector(i)
                     for call in newton[0:1]:
@@ -434,7 +434,8 @@ def tile_frozenhopfield_pa_kernel(tc, q, word_embs, beta, out):
                         spread_query_norms()
                     if now and fresh:
                         quantise_regrouped(*side)
-                keep_and_max(GROUPS - 1)
+                quantise_regrouped(GROUPS - 2, 1)
+                keep_and_min(GROUPS - 1)
 
             with (
                 tc.tile_pool(name="late", bufs=1) as late,
@@ -446,10 +447,8 @@ def tile_frozenhopfield_pa_kernel(tc, q, word_embs, beta, out):
                 p_codes = late.tile([P, GROUPS, QUERIES], U32, align_bytes=64)
                 p_scales = late.tile([P, GROUPS, QUERIES], U8, align_bytes=64)
                 neg_max = late.tile([P, Q_TILES], F32)
-                nc.vector.tensor_reduce(out=neg_max[:], in_=part_max[:], axis=AXIS.X, op=ALU.max)
-                nc.vector.tensor_scalar_mul(out=neg_max[:], in0=neg_max[:], scalar1=-1.0)
-                for g in (GROUPS - 2, GROUPS - 1):
-                    quantise_regrouped(g, 1)
+                nc.vector.tensor_reduce(out=neg_max[:], in_=part_min[:], axis=AXIS.X, op=ALU.min)
+                quantise_regrouped(GROUPS - 1, 1)
                 acc = {}
                 for t in range(Q_TILES):
                     for hh in range(H_HALVES):
@@ -468,7 +467,7 @@ def tile_frozenhopfield_pa_kernel(tc, q, word_embs, beta, out):
                             in_=x_sb[:, t, cols],
                             func=ACT.Exp,
                             bias=neg_max[:, t : t + 1],
-                            scale=1.0,
+                            scale=-1.0,
                             accum_out=part_sum[:, t, u : u + 1],
                         )
 
@@ -522,7 +521,7 @@ def tile_frozenhopfield_pa_kernel(tc, q, word_embs, beta, out):
                     if u + 1 < len(UNITS) and u >= 0:
                         exponentials(u + 1)
                     for g in batch:
-                        if u >= 0:
+                        if g != LATE_PAIRS[0][0]:
                             regroup(g, 1)
                     if u >= 0:
                         turn_probs(u)

@@ -30,8 +30,8 @@ EPS = 1e-8
 TINY = 1e-30
 GRAM = (3,)
 BANKS = [(c, jp) for c in range(H_PASSES) for jp in range(PACK // 2)]
-ROWS_ON_SCALAR = (1, 0)
-ROWS_ON_VECTOR = (0, 1)
+ROWS_ON_SCALAR = 0
+ROWS_ON_VECTOR = 0
 EARLY = 2
 LATE_PAIRS = tuple((g, g + 1) for g in range(EARLY, GROUPS - 2, 2))
 
@@ -229,7 +229,7 @@ def tile_frozenhopfield_pa_kernel(tc, q, word_embs, beta, out):
 
                 def factors_on_scalar(g):
                     r, r_sq = recip[g]
-                    for j in range(ROWS_ON_SCALAR[g % 2]):
+                    for j in range(ROWS_ON_SCALAR):
                         nc.scalar.activation(
                             out=g_t[g][:, j, :],
                             in_=neg_c_rows[:],
@@ -240,7 +240,7 @@ def tile_frozenhopfield_pa_kernel(tc, q, word_embs, beta, out):
 
                 def factors_on_vector(g):
                     r, r_sq = recip[g]
-                    for j in range(PACK - ROWS_ON_VECTOR[g % 2], PACK):
+                    for j in range(PACK - ROWS_ON_VECTOR, PACK):
                         nc.vector.tensor_scalar(
                             out=g_t[g][:, j, :],
                             in0=neg_c_rows[:],
@@ -252,7 +252,7 @@ def tile_frozenhopfield_pa_kernel(tc, q, word_embs, beta, out):
 
                 def factors_on_gpsimd(g):
                     r, r_sq = recip[g]
-                    for j in range(ROWS_ON_SCALAR[g % 2], PACK - ROWS_ON_VECTOR[g % 2]):
+                    for j in range(ROWS_ON_SCALAR, PACK - ROWS_ON_VECTOR):
                         nc.gpsimd.tensor_scalar(
                             out=g_t[g][:, j, :],
                             in0=neg_c_rows[:],
@@ -413,15 +413,13 @@ def tile_frozenhopfield_pa_kernel(tc, q, word_embs, beta, out):
                         keep_and_min(i - 1)
                     if now:
                         factors_on_vector(i)
+                    if now:
+                        normalise(i, 0)
                     for call in newton[0:1]:
                         call()
                     if now and fresh:
                         regroup(*side)
                     for call in newton[1:2]:
-                        call()
-                    if now:
-                        normalise(i, 0)
-                    for call in newton[2:3]:
                         call()
                     if now:
                         normalise(i, 1)
@@ -430,6 +428,8 @@ def tile_frozenhopfield_pa_kernel(tc, q, word_embs, beta, out):
                         first_products(i + 1)
                     if fresh:
                         gram_diagonals(i + 2)
+                    for call in newton[2:3]:
+                        call()
                     if not now:
                         spread_query_norms()
                     if now and fresh:

import concourse.mybir as mybir
from concourse.masks import make_identity

FLOPS = 2 * 2 * 256 * 8192 * 1024

F32 = mybir.dt.float32
BF16 = mybir.dt.bfloat16
U32 = mybir.dt.uint32
U8 = mybir.dt.uint8
FP8X4 = mybir.dt.float8_e4m3fn_x4
ALU = mybir.AluOpType
ACT = mybir.ActivationFunctionType
AXIS = mybir.AxisListType

P = 128
PACK = 4
K_PASS = P * PACK
BANK = 512

QUERIES = 256
HID = 1024
VOCAB = 8192
Q_TILES = QUERIES // P
H_PASSES = HID // K_PASS
GROUPS = VOCAB // K_PASS
H_HALVES = HID // BANK
PAIR = 2
UNITS = [(g, g + 1) for g in range(0, GROUPS - PAIR, PAIR)] + [(GROUPS - 2,), (GROUPS - 1,)]
EPS = 1e-8
TINY = 1e-30
GRAM = (3,)
BANKS = [(c, jp) for c in range(H_PASSES) for jp in range(PACK // 2)]
ROWS_ON_SCALAR = 0
ROWS_ON_VECTOR = 0
EARLY = 2
LATE_PAIRS = tuple((g, g + 1) for g in range(EARLY, GROUPS - 2, 2))


def tile_frozenhopfield_pa_kernel(tc, q, word_embs, beta, out):
    nc = tc.nc
    with tc.tile_pool(name="keep", bufs=1) as keep, tc.tile_pool(name="stream", bufs=3) as stream, tc.tile_pool(
        name="regroup", bufs=4
    ) as regroup_pool, tc.tile_pool(name="stats", bufs=4) as stats:
        ident_f = keep.tile([P, P], F32)
        make_identity(nc, ident_f[:])

        warm = keep.tile([P, 1], F32)
        nc.vector.memset(warm[:], 1.0)
        nc.scalar.activation(out=warm[:], in_=warm[:], func=ACT.Abs_reciprocal_sqrt, bias=TINY)

        x_sb = keep.tile([P, Q_TILES, VOCAB], F32)
        e2_codes = keep.tile([P, GROUPS, HID], U32, align_bytes=64)
        e2_scales = keep.tile([P, GROUPS, HID], U8, align_bytes=64)
        q_codes = keep.tile([P, H_PASSES, QUERIES], U32, align_bytes=64)
        q_scales = keep.tile([P, H_PASSES, QUERIES], U8, align_bytes=64)
        neg_c_rows = keep.tile([P, QUERIES], F32)
        x_scale = keep.tile([P, Q_TILES], F32)
        neg_c = keep.tile([P, Q_TILES], F32)
        part_min = keep.tile([P, Q_TILES, GROUPS], F32)
        part_sum = keep.tile([P, Q_TILES, len(UNITS)], F32, name="part_sum")

        e_raw = {}
        e_half = {}
        regrouped = {}

        def word_rows(g):
            return word_embs[g * K_PASS : (g + 1) * K_PASS, :].rearrange("(p j) h -> p j h", j=PACK)

        def load(g, pieces=1):
            e_raw[g] = stream.tile([P, PACK, HID], BF16, name="e_raw")
            n = HID // pieces
            for k in range(pieces):
                nc.sync.dma_start(out=e_raw[g][:, :, k * n : (k + 1) * n], in_=word_rows(g)[:, :, k * n : (k + 1) * n])

        def load_late(pair):
            both = stream.tile([P, 2, PACK, BANK], BF16, name="e_half", tag="e_raw")
            for k, g in enumerate(pair):
                nc.sync.dma_start(out=both[:, k, :, :], in_=word_rows(g)[:, :, BANK:HID])
                e_half[g] = both[:, k, :, :]

        def regroup(g, hh, copy=nc.vector.tensor_copy):
            regrouped[(g, hh)] = regroup_pool.tile([P, BANK, PACK], BF16, name="e_regrouped", align_bytes=64)
            rows = e_half[g] if g in e_half else e_raw[g][:, :, hh * BANK : (hh + 1) * BANK]
            copy(
                out=regrouped[(g, hh)][:].rearrange("p (c i) t -> p c t i", i=4),
                in_=rows.rearrange("p t (c i) -> p c t i", i=4),
            )

        def quantise_regrouped(g, hh):
            cols = slice(hh * BANK, (hh + 1) * BANK)
            nc.vector.quantize_mx(
                out=e2_codes[:, g, cols].bitcast(FP8X4),
                scales=e2_scales[:, g, cols],
                in_=regrouped[(g, hh)][:].rearrange("p h t -> p (h t)"),
            )

        def rough_reciprocal_norm(sum_sq, width):
            rough = stats.tile([P, width], F32)
            nc.scalar.activation(out=rough[:], in_=sum_sq, func=ACT.Abs_reciprocal_sqrt, bias=TINY)
            return rough

        def newton_steps(sum_sq, rough, width):
            factor = stats.tile([P, width], F32)
            recip = stats.tile([P, width], F32)
            recip_sq = stats.tile([P, width], F32)
            calls = [
                lambda: nc.vector.scalar_tensor_tensor(
                    out=factor[:], in0=rough[:], scalar=-0.5, in1=rough[:], op0=ALU.mult, op1=ALU.mult
                ),
                lambda: nc.vector.tensor_mul(out=factor[:], in0=factor[:], in1=sum_sq),
                lambda: nc.vector.scalar_tensor_tensor(
                    out=recip[:], in0=factor[:], scalar=1.5, in1=rough[:], op0=ALU.add, op1=ALU.mult
                ),
                lambda: nc.vector.tensor_mul(out=recip_sq[:], in0=recip[:], in1=recip[:]),
            ]
            return calls, recip, recip_sq

        with tc.manual_schedule():
            with (
                tc.tile_pool(name="work", bufs=2) as work,
                tc.psum_pool(name="ps_xt", bufs=3) as ps_xt,
                tc.psum_pool(name="ps_gram", bufs=1) as ps_gram,
                tc.psum_pool(name="ps_st", bufs=2) as ps_st,
                tc.psum_pool(name="ps_yn", bufs=2) as ps_yn,
            ):
                e_sq = {}
                gram = {}
                last_newton = {}
                rough = {}
                recip = {}
                turned_words = {}
                g1 = {}
                e1 = {}
                st = {}
                g_t = {}
                y_t = {}
                y_n = {}

                def turn_words(g, banks):
                    e_words = e_raw[g][:].bitcast(F32)
                    for c, jp in banks:
                        xt = ps_xt.tile([P, 2, 2 * P], F32, tag="xt")
                        for u in range(2):
                            for jj in range(2):
                                w0 = (2 * c + u) * P
                                nc.tensor.transpose(
                                    xt[:, u, jj * P : (jj + 1) * P], e_words[:, 2 * jp + jj, w0 : w0 + P], ident_f[:]
                                )
                        turned_words[(g, c, jp)] = xt

                def copy_words(g, banks):
                    for c, jp in banks:
                        if (c, jp) == BANKS[0]:
                            g1[g] = work.tile([P, H_PASSES, K_PASS, PACK], BF16, name="g1", align_bytes=64)
                        nc.scalar.copy(
                            out=g1[g][:].bitcast(F32)[:, c, jp * 2 * P : (jp + 1) * 2 * P, :],
                            in_=turned_words[(g, c, jp)][:].rearrange("p u v -> p v u"),
                        )


                def gram_products(g):
                    gram[g] = ps_gram.tile([P, 2, P], F32, name="gram")
                    for k, j in enumerate(GRAM):
                        for c in range(H_PASSES):
                            for t in range(PACK):
                                part = g1[g][:, c, j * P : (j + 1) * P, t]
                                nc.tensor.matmul(
                                    out=gram[g][:, k, :],
                                    lhsT=part,
                                    rhs=part,
                                    start=(c == 0 and t == 0),
                                    stop=(c == H_PASSES - 1 and t == PACK - 1),
                                )

                def gram_diagonals(g):
                    for k, j in enumerate(GRAM):
                        diagonal = work.tile([P, P], BF16)
                        nc.vector.scalar_tensor_tensor(
                            out=diagonal[:],
                            in0=gram[g][:, k, :],
                            scalar=1.0,
                            in1=ident_f[:],
                            op0=ALU.mult,
                            op1=ALU.mult,
                            accum_out=e_sq[g][:, j : j + 1],
                        )

                def squared_norms(g):
                    e_sq[g] = stats.tile([P, PACK], F32, name="e_sq")
                    for j in range(PACK):
                        if j in GRAM:
                            continue
                        junk = work.tile([P, HID], BF16, tag="junk")
                        nc.scalar.activation(
                            out=junk[:], in_=e_raw[g][:, j, :], func=ACT.Square, accum_out=e_sq[g][:, j : j + 1]
                        )

                def quantise_words(g):
                    codes = work.tile([P, H_PASSES, K_PASS], U32, name="e1_codes", align_bytes=64)
                    scales = work.tile([P, H_PASSES, K_PASS], U8, name="e1_scales", align_bytes=64)
                    e1[g] = (codes, scales)
                    nc.vector.quantize_mx(
                        out=codes[:].rearrange("p c v -> p (c v)").bitcast(FP8X4),
                        scales=scales[:].rearrange("p c v -> p (c v)"),
                        in_=g1[g][:].rearrange("p c v t -> p (c v t)"),
                    )

                def first_products(g):
                    codes, scales = e1[g]
                    st[g] = []
                    for jp in range(PACK // 2):
                        s_t = ps_st.tile([P, 2, QUERIES], F32, tag="st")
                        for jj in range(2):
                            j = 2 * jp + jj
                            for c in range(H_PASSES):
                                nc.tensor.matmul_mx(
                                    out=s_t[:, jj, :],
                                    lhsT=codes[:, c, j * P : (j + 1) * P].bitcast(FP8X4),
                                    lhsT_scale=scales[:, c, j * P : (j + 1) * P],
                                    rhs=q_codes[:, c, :].bitcast(FP8X4),
                                    rhs_scale=q_scales[:, c, :],
                                    start=(c == 0),
                                    stop=(c == H_PASSES - 1),
                                )
                        st[g].append(s_t)

                def start_factors(g):
                    g_t[g] = work.tile([P, PACK, QUERIES], F32, name="g_t", align_bytes=64)

                def factors_on_scalar(g):
                    r, r_sq = recip[g]
                    for j in range(ROWS_ON_SCALAR):
                        nc.scalar.activation(
                            out=g_t[g][:, j, :],
                            in_=neg_c_rows[:],
                            func=ACT.Identity,
                            scale=r_sq[:, j : j + 1],
                            bias=r[:, j : j + 1],
                        )

                def factors_on_vector(g):
                    r, r_sq = recip[g]
                    for j in range(PACK - ROWS_ON_VECTOR, PACK):
                        nc.vector.tensor_scalar(
                            out=g_t[g][:, j, :],
                            in0=neg_c_rows[:],
                            scalar1=r_sq[:, j : j + 1],
                            scalar2=r[:, j : j + 1],
                            op0=ALU.mult,
                            op1=ALU.add,
                        )

                def factors_on_gpsimd(g):
                    r, r_sq = recip[g]
                    for j in range(ROWS_ON_SCALAR, PACK - ROWS_ON_VECTOR):
                        nc.gpsimd.tensor_scalar(
                            out=g_t[g][:, j, :],
                            in0=neg_c_rows[:],
                            scalar1=r_sq[:, j : j + 1],
                            scalar2=r[:, j : j + 1],
                            op0=ALU.mult,
                            op1=ALU.add,
                        )

                def normalise(g, jp):
                    if jp == 0:
                        y_t[g] = work.tile([P, PACK, QUERIES], F32, name="y_t")
                    js = slice(2 * jp, 2 * jp + 2)
                    nc.vector.tensor_tensor(out=y_t[g][:, js, :], in0=st[g][jp][:], in1=g_t[g][:, js, :], op=ALU.mult)

                def turn_scores(g):
                    y_n[g] = []
                    for t in range(Q_TILES):
                        turned = ps_yn.tile([P, BANK], F32, tag="yn")
                        for j in range(PACK):
                            nc.tensor.transpose(turned[:, j * P : (j + 1) * P], y_t[g][:, j, t * P : (t + 1) * P], ident_f[:])
                        y_n[g].append(turned)

                def keep_and_min(g):
                    for t in range(Q_TILES):
                        nc.vector.tensor_scalar(
                            out=x_sb[:, t, g * K_PASS : (g + 1) * K_PASS].rearrange("p (u w e) -> p u w e", u=2, e=2),
                            in0=y_n[g][t][:].rearrange("p (u e w) -> p u w e", u=2, e=2),
                            scalar1=x_scale[:, t : t + 1],
                            scalar2=None,
                            op0=ALU.mult,
                            op1=ALU.min,
                            accum_out=part_min[:, t, g : g + 1],
                        )

                load(0, pieces=H_HALVES)
                q_raw = work.tile([P, Q_TILES, HID], BF16, tag="y_t")
                nc.sync.dma_start(out=q_raw[:], in_=q.rearrange("(t p) h -> p t h", p=P))
                load(1)
                load(2)

                turn_words(0, BANKS[:3])
                copy_words(0, BANKS[:1])
                turn_words(0, BANKS[3:])
                copy_words(0, BANKS[1:])
                regroup(0, 0)
                regroup(0, 1)

                q_words = q_raw[:].bitcast(F32)
                q_grouped = work.tile([P, H_PASSES, QUERIES, PACK], BF16, tag="g_t", align_bytes=64)
                for c in range(H_PASSES):
                    xt = ps_xt.tile([P, 2, QUERIES], F32, tag="xt")
                    for u in range(2):
                        for t in range(Q_TILES):
                            w0 = (2 * c + u) * P
                            nc.tensor.transpose(xt[:, u, t * P : (t + 1) * P], q_words[:, t, w0 : w0 + P], ident_f[:])
                    nc.scalar.copy(out=q_grouped[:].bitcast(F32)[:, c, :, :], in_=xt[:].rearrange("p u b -> p b u"))
                turn_words(1, BANKS[:3])
                gram_products(0)

                q_sq = stats.tile([P, Q_TILES], F32)
                for t in range(Q_TILES):
                    junk = work.tile([P, HID], BF16, tag="junk")
                    nc.vector.scalar_tensor_tensor(
                        out=junk[:],
                        in0=q_raw[:, t, :],
                        scalar=1.0,
                        in1=q_raw[:, t, :],
                        op0=ALU.mult,
                        op1=ALU.mult,
                        accum_out=q_sq[:, t : t + 1],
                    )
                q_rough = rough_reciprocal_norm(q_sq[:], Q_TILES)
                squared_norms(0)

                quantise_regrouped(0, 0)
                quantise_words(0)
                quantise_regrouped(0, 1)
                nc.vector.quantize_mx(
                    out=q_codes[:].rearrange("p c b -> p (c b)").bitcast(FP8X4),
                    scales=q_scales[:].rearrange("p c b -> p (c b)"),
                    in_=q_grouped[:].rearrange("p c b t -> p (c b t)"),
                )
                first_products(0)
                gram_diagonals(0)
                q_newton, q_recip, q_recip_sq = newton_steps(q_sq[:], q_rough, Q_TILES)
                for call in q_newton[:1]:
                    call()
                regroup(1, 0)
                for call in q_newton[1:2]:
                    call()
                regroup(1, 1)
                for call in q_newton[2:3]:
                    call()
                quantise_regrouped(1, 0)
                nc.vector.tensor_scalar_mul(out=neg_c[:], in0=q_recip[:], scalar1=-EPS)
                nc.vector.tensor_scalar_mul(out=x_scale[:], in0=q_recip[:], scalar1=-float(beta))
                quantise_regrouped(1, 1)


                def spread_query_norms():
                    c_ps = ps_yn.tile([P, QUERIES], F32, tag="yn")
                    for t in range(Q_TILES):
                        nc.tensor.matmul(
                            out=c_ps[:, t * P : (t + 1) * P],
                            lhsT=neg_c[:, t : t + 1].to_broadcast([P, P]),
                            rhs=ident_f[:],
                            start=True,
                            stop=True,
                        )
                    nc.vector.tensor_copy(out=neg_c_rows[:], in_=c_ps[:])

                load(3)

                for i in range(-1, GROUPS):
                    now = i >= 0
                    ahead = i + 1 < GROUPS
                    fresh = i + 2 < GROUPS
                    side = (i + 2, 0) if fresh else (i, 1)
                    if now:
                        if i + 4 < GROUPS:
                            load(i + 4)
                        elif i + 4 == GROUPS:
                            load_late(LATE_PAIRS[0])

                    if fresh:
                        turn_words(i + 2, BANKS[3:])
                        copy_words(i + 2, BANKS[:1])
                    if ahead:
                        rough[i + 1] = rough_reciprocal_norm(e_sq[i + 1][:], PACK)
                        newton, r, r_sq = newton_steps(e_sq[i + 1][:], rough[i + 1], PACK)
                        recip[i + 1] = (r, r_sq)
                        last_newton[i + 1] = newton[3]
                    else:
                        newton = []
                    if fresh:
                        copy_words(i + 2, BANKS[1:])
                        gram_products(i + 2)
                    if i + 3 < GROUPS:
                        turn_words(i + 3, BANKS[:3])
                    if now:
                        last_newton[i]()
                    if ahead and now:
                        quantise_words(i + 1)
                    if now:
                        start_factors(i)
                        factors_on_scalar(i)
                        factors_on_gpsimd(i)
                    if i == GROUPS - 2:
                        for g in (GROUPS - 2, GROUPS - 1):
                            regroup(g, 1, nc.scalar.copy)
                    if i == GROUPS - 1:
                        nc.scalar.activation(out=warm[:], in_=warm[:], func=ACT.Exp)
                        regroup(LATE_PAIRS[0][0], 1, nc.scalar.copy)
                    if fresh:
                        squared_norms(i + 2)
                    if i > 0:
                        keep_and_min(i - 1)
                    if now:
                        factors_on_vector(i)
                    if now:
                        normalise(i, 0)
                    for call in newton[0:1]:
                        call()
                    if now and fresh:
                        regroup(*side)
                    for call in newton[1:2]:
                        call()
                    if now:
                        normalise(i, 1)
                        turn_scores(i)
                    if ahead and now:
                        first_products(i + 1)
                    if fresh:
                        gram_diagonals(i + 2)
                    for call in newton[2:3]:
                        call()
                    if not now:
                        spread_query_norms()
                    if now and fresh:
                        quantise_regrouped(*side)
                quantise_regrouped(GROUPS - 2, 1)
                keep_and_min(GROUPS - 1)

            with (
                tc.tile_pool(name="late", bufs=1) as late,
                tc.tile_pool(name="probs", bufs=4) as probs,
                tc.tile_pool(name="turned", bufs=2) as turned_pool,
                tc.psum_pool(name="ps_acc", bufs=1) as ps_acc,
                tc.psum_pool(name="ps_pt", bufs=4) as ps_pt,
            ):
                p_codes = late.tile([P, GROUPS, QUERIES], U32, align_bytes=64)
                p_scales = late.tile([P, GROUPS, QUERIES], U8, align_bytes=64)
                neg_max = late.tile([P, Q_TILES], F32)
                nc.vector.tensor_reduce(out=neg_max[:], in_=part_min[:], axis=AXIS.X, op=ALU.min)
                quantise_regrouped(GROUPS - 1, 1)
                acc = {}
                for t in range(Q_TILES):
                    for hh in range(H_HALVES):
                        acc[(t, hh)] = ps_acc.tile([P, BANK], F32, name="acc%d%d" % (t, hh))

                p_bf = {}
                p_grouped = {}

                def exponentials(u):
                    cols = slice(UNITS[u][0] * K_PASS, (UNITS[u][-1] + 1) * K_PASS)
                    width = len(UNITS[u]) * K_PASS
                    for t in range(Q_TILES):
                        p_bf[(u, t)] = probs.tile([P, PAIR * K_PASS], BF16, name="p_bf")
                        nc.scalar.activation(
                            out=p_bf[(u, t)][:, 0:width],
                            in_=x_sb[:, t, cols],
                            func=ACT.Exp,
                            bias=neg_max[:, t : t + 1],
                            scale=-1.0,
                            accum_out=part_sum[:, t, u : u + 1],
                        )

                def turn_probs(u):
                    p_grouped[u] = turned_pool.tile([P, PAIR, QUERIES, PACK], BF16, name="p_grouped", align_bytes=64)
                    for gl in range(len(UNITS[u])):
                        p_t = ps_pt.tile([P, 2, QUERIES], F32, tag="pt")
                        for half in range(2):
                            for t in range(Q_TILES):
                                w0 = (gl * 2 + half) * P
                                p_words = p_bf[(u, t)][:].bitcast(F32)
                                nc.tensor.transpose(p_t[:, half, t * P : (t + 1) * P], p_words[:, w0 : w0 + P], ident_f[:])
                        copy_out = nc.vector.tensor_copy if u == 0 else nc.scalar.copy
                        copy_out(
                            out=p_grouped[u][:].bitcast(F32)[:, gl, :, :],
                            in_=p_t[:].rearrange("p k b -> p b k"),
                        )

                def quantise_probs(u):
                    gs = slice(UNITS[u][0], UNITS[u][-1] + 1)
                    nc.vector.quantize_mx(
                        out=p_codes[:, gs, :].rearrange("p g b -> p (g b)").bitcast(FP8X4),
                        scales=p_scales[:, gs, :].rearrange("p g b -> p (g b)"),
                        in_=p_grouped[u][:, 0 : len(UNITS[u]), :, :].rearrange("p g b t -> p (g b t)"),
                    )

                def second_products(u):
                    for t in range(Q_TILES):
                        for g in UNITS[u]:
                            for hh in range(H_HALVES):
                                nc.tensor.matmul_mx(
                                    out=acc[(t, hh)][:],
                                    lhsT=p_codes[:, g, t * P : (t + 1) * P].bitcast(FP8X4),
                                    lhsT_scale=p_scales[:, g, t * P : (t + 1) * P],
                                    rhs=e2_codes[:, g, hh * BANK : (hh + 1) * BANK].bitcast(FP8X4),
                                    rhs_scale=e2_scales[:, g, hh * BANK : (hh + 1) * BANK],
                                    start=(g == 0),
                                    stop=(g == GROUPS - 1),
                                )

                load_late(LATE_PAIRS[1])
                load_late(LATE_PAIRS[2])
                exponentials(0)
                halves = [g for pair in LATE_PAIRS for g in pair]
                loads = 3
                done = 0
                for u in range(-1, len(UNITS)):
                    share = 2 if u in (-1, 0, 1, 4) else 1
                    batch = halves[done : done + share]
                    done += share
                    if u + 1 < len(UNITS) and u >= 0:
                        exponentials(u + 1)
                    for g in batch:
                        if g != LATE_PAIRS[0][0]:
                            regroup(g, 1)
                    if u >= 0:
                        turn_probs(u)
                        quantise_probs(u)
                    for g in batch:
                        quantise_regrouped(g, 1)
                    if loads < len(LATE_PAIRS) and done >= 2 * (loads - 2):
                        load_late(LATE_PAIRS[loads])
                        loads += 1
                    if u >= 2:
                        second_products(u - 2)
                row_sum = late.tile([P, Q_TILES], F32)
                nc.vector.tensor_reduce(out=row_sum[:], in_=part_sum[:], axis=AXIS.X, op=ALU.add)
                inv_sum = late.tile([P, Q_TILES], F32)
                nc.vector.reciprocal(out=inv_sum[:], in_=row_sum[:])
                second_products(len(UNITS) - 2)
                second_products(len(UNITS) - 1)
                for t in range(Q_TILES):
                    for hh in range(H_HALVES):
                        result = turned_pool.tile([P, BANK], F32, name="result%d" % hh)
                        if hh == 0:
                            nc.vector.tensor_scalar_mul(out=result[:], in0=acc[(t, hh)][:], scalar1=inv_sum[:, t : t + 1])
                        else:
                            nc.scalar.activation(out=result[:], in_=acc[(t, hh)][:], func=ACT.Copy, scale=inv_sum[:, t : t + 1])
                        nc.sync.dma_start(out=out[t * P : (t + 1) * P, hh * BANK : (hh + 1) * BANK], in_=result[:])
